import numpy as np
import ml_dtypes


def mxq(x, axis, fmt="e4m3"):
    dtype, down = {"e4m3": (ml_dtypes.float8_e4m3fn, 7), "e5m2": (ml_dtypes.float8_e5m2, 14)}[fmt]
    v = np.moveaxis(np.asarray(x, np.float32).astype(ml_dtypes.bfloat16).astype(np.float64), axis, -1)
    blocks = v.reshape(v.shape[:-1] + (-1, 32))
    amax = np.abs(blocks).max(-1, keepdims=True)
    byte = np.maximum(np.where(amax > 0, np.frexp(amax)[1] - 1 + 127, 0) - down, 1)
    scale = np.exp2(byte - 127.0)
    codes = (blocks / scale).astype(np.float32).astype(dtype).astype(np.float64)
    return np.moveaxis((codes * scale).reshape(v.shape), -1, axis)


WIDE = False


def mx_kscale(k):
    if not WIDE:
        return np.ones(k)
    levels = np.array([10, -10, 5, -5, 0])
    if k % 512:
        return np.exp2(np.random.permutation(np.resize(levels, k // 32))).repeat(32)
    a = np.empty((k // 512, 16))
    for p in range(k // 512):
        a[p, :8] = np.random.permutation(np.resize(levels, 8))
        for g in range(8):
            far = levels[np.abs(levels - a[p, g]) >= 10]
            a[p, g + 8] = far[np.random.randint(len(far))]
    return np.exp2(a.ravel()).repeat(32)


BF16 = ml_dtypes.bfloat16


def bf(x):
    return np.asarray(x, np.float32).astype(BF16)


def f64(x):
    return np.asarray(x).astype(np.float64)


B, S, D, H, DC, DR = 4, 1024, 512, 16, 512, 64
HALF = DR // 2
ROPE_BASE = 10000.0


def rope_tables():
    inv_freq = 1.0 / ROPE_BASE ** (np.arange(0, DR, 2) / DR)
    ang = np.arange(S)[:, None] * inv_freq[None, :]
    return np.cos(ang), np.sin(ang)


def setup_inputs():
    s = mx_kscale(D)
    t = np.array(mx_kscale(DC), dtype=np.float64)
    t[HALF:DR] = t[:HALF]
    return {"x": bf(np.random.standard_normal((B, S, D)) * s),
            "W_c": bf(np.random.standard_normal((D, DC)) / np.sqrt(D) / s[:, None] * t),
            "b_c": bf(np.random.standard_normal(DC) * 0.3 * t),
            "W_d": bf(np.random.standard_normal((DC, 3 * D)) / np.sqrt(DC) / t[:, None]),
            "b_d": bf(np.random.standard_normal(3 * D) * 0.3)}


def reference(x, W_c, b_c, W_d, b_d):
    cos, sin = rope_tables()
    c = (mxq(f64(x), 2, "e4m3") @ mxq(f64(W_c), 0, "e4m3")) + f64(b_c)
    c1, c2 = c[..., :HALF], c[..., HALF:DR]
    c = np.concatenate([c1 * cos - c2 * sin, c1 * sin + c2 * cos, c[..., DR:]], axis=-1)
    return (mxq(c, 2, "e4m3") @ mxq(f64(W_d), 0, "e4m3")) + f64(b_d)

@@ -1,0 +1,296 @@
+import math
+from contextlib import ExitStack
+
+import concourse.mybir as mybir
+from concourse.masks import make_identity
+
+F32 = mybir.dt.float32
+BF16 = mybir.dt.bfloat16
+I32 = mybir.dt.int32
+U32 = mybir.dt.uint32
+U8 = mybir.dt.uint8
+FP8X4 = mybir.dt.float8_e4m3fn_x4
+ADD = mybir.AluOpType.add
+SUBTRACT = mybir.AluOpType.subtract
+MULT = mybir.AluOpType.mult
+SIN = mybir.ActivationFunctionType.Sin
+
+B, S, D, DC, DR, OUT = 4, 1024, 512, 512, 64, 1536
+HALF = DR // 2
+ROPE_BASE = 10000.0
+
+P = 128
+PACK = 4
+TILES = 4
+GROUP = TILES * P
+GROUPS = B * S // GROUP
+GROUPS_PER_SEQUENCE = S // GROUP
+BANK = 512
+OUT_BANKS = OUT // BANK
+ROT_P = DR // PACK
+PAIRED = 2 * DR
+ROUND_MAGIC = 1.5 * 2.0**23
+LAG_C, LAG_R, LAG_OUT = 1, 2, 3
+RESULT_BUFS = 2 * TILES
+TWO_BANK_TILES = 4
+
+FLOPS = 2 * B * S * D * DC + 2 * B * S * DC * OUT
+
+
+def append_partners(engine, cols):
+    slots = cols[:, 0:DC, :].rearrange("q (t p) w -> q t p w", t=PACK)
+    paired = cols[:, DC : DC + PAIRED, :].rearrange("q (s t p) w -> q s t p w", s=2, t=PACK)
+    far = ROT_P // 2
+    engine.tensor_copy(out=paired[:, 0], in_=slots[:, :, 0:ROT_P, :])
+    engine.tensor_copy(out=paired[:, 1, :, 0:far, :], in_=slots[:, :, far:ROT_P, :])
+    engine.tensor_copy(out=paired[:, 1, :, far:ROT_P, :], in_=slots[:, :, 0:far, :])
+
+
+def tile_deepseekmla_pa_t_kernel(tc, x, W_c, b_c, W_d, b_d, out):
+    nc = tc.nc
+    x_groups = x.flatten_outer_dims().rearrange("(g p a) d -> g p (a d)", p=P, a=TILES)
+    out_groups = out.flatten_outer_dims().rearrange("(g p a) c -> g p a c", p=P, a=TILES)
+
+    with ExitStack() as ctx:
+        consts = ctx.enter_context(tc.tile_pool(name="consts", bufs=1))
+        work = ctx.enter_context(tc.tile_pool(name="work", bufs=3))
+        results = ctx.enter_context(tc.tile_pool(name="results", bufs=RESULT_BUFS))
+        front_psum = ctx.enter_context(tc.psum_pool(name="front_psum", bufs=4))
+        out_psum = ctx.enter_context(tc.psum_pool(name="out_psum", bufs=4))
+        ctx.enter_context(tc.manual_schedule())
+
+        wc_raw = consts.tile([P, PACK, DC], BF16)
+        nc.sync.dma_start(
+            out=wc_raw[:],
+            in_=W_c.rearrange("(q k) c -> q k c", k=PACK),
+        )
+        x_sb = []
+        for g in range(GROUPS):
+            x_sb.append(consts.tile([P, TILES * D], BF16, name="x_sb%d" % g))
+        bc_raw = consts.tile([P, DC], BF16)
+        nc.sync.dma_start(out=bc_raw[:], in_=b_c.partition_broadcast(P))
+        for g in range(2):
+            nc.sync.dma_start(out=x_sb[g][:], in_=x_groups[g])
+        wd_raw = consts.tile([P, PACK, OUT], BF16)
+        wd_rows = W_d.rearrange("(p t) c -> p t c", t=PACK)
+        for n in range(OUT_BANKS):
+            nc.sync.dma_start(
+                out=wd_raw[:, :, n * BANK : (n + 1) * BANK],
+                in_=wd_rows[:, :, n * BANK : (n + 1) * BANK],
+            )
+        bd_all = consts.tile([P, OUT], BF16)
+        nc.sync.dma_start(out=bd_all[:], in_=b_d.partition_broadcast(P))
+        for g in range(2, GROUPS):
+            nc.sync.dma_start(out=x_sb[g][:], in_=x_groups[g])
+
+        position = consts.tile([P, GROUPS_PER_SEQUENCE * TILES, 1], I32)
+        nc.gpsimd.iota(
+            position[:], pattern=[[GROUP, GROUPS_PER_SEQUENCE], [1, TILES]], base=0, channel_multiplier=TILES
+        )
+        ident_f32 = consts.tile([P, P], F32)
+        make_identity(nc, ident_f32[:])
+        ident_bf16 = consts.tile([P, P], BF16)
+        make_identity(nc, ident_bf16[:])
+        turns = consts.tile([P, 2, GROUPS_PER_SEQUENCE * TILES, HALF], F32)
+        for j in range(HALF):
+            column = (j % PACK) * (HALF // PACK) + j // PACK
+            nc.vector.tensor_scalar_mul(
+                out=turns[:, 0, :, column : column + 1],
+                in0=position[:],
+                scalar1=1.0 / ROPE_BASE ** (2.0 * j / DR) / (2.0 * math.pi),
+            )
+
+        wc_grouped = consts.tile([P, DC + PAIRED, PACK], BF16, align_bytes=64)
+        nc.vector.tensor_copy(
+            out=wc_grouped[:, 0:DC, :].rearrange("q (t p) k -> q t p k", t=PACK),
+            in_=wc_raw[:].rearrange("q k (p t) -> q t p k", t=PACK),
+        )
+        append_partners(nc.vector, wc_grouped[:])
+        wc_codes = consts.tile([P, DC + PAIRED], U32, align_bytes=64)
+        wc_scales = consts.tile([P, DC + PAIRED], U8, align_bytes=64)
+        for cols in (slice(0, DC), slice(DC, DC + PAIRED)):
+            nc.vector.quantize_mx(
+                out=wc_codes[:, cols].bitcast(FP8X4),
+                scales=wc_scales[:, cols],
+                in_=wc_grouped[:, cols, :].rearrange("q c k -> q (c k)"),
+            )
+        bc_cols = consts.tile([P, DC + PAIRED, 1], F32)
+        nc.gpsimd.tensor_copy(
+            out=bc_cols[:, 0:DC, 0].rearrange("q (t p) -> q t p", t=PACK),
+            in_=bc_raw[:].rearrange("q (p t) -> q t p", t=PACK),
+        )
+        append_partners(nc.gpsimd, bc_cols[:])
+
+        nc.vector.tensor_scalar_add(out=turns[:, 1], in0=turns[:, 0], scalar1=0.25)
+        whole = consts.tile([P, 2, GROUPS_PER_SEQUENCE * TILES, HALF], F32)
+        nc.vector.tensor_scalar(
+            out=whole[:], in0=turns[:], scalar1=ROUND_MAGIC, scalar2=ROUND_MAGIC, op0=ADD, op1=SUBTRACT
+        )
+        nc.vector.tensor_tensor(out=turns[:], in0=turns[:], in1=whole[:], op=SUBTRACT)
+        table = consts.tile([P, GROUPS_PER_SEQUENCE * TILES, PAIRED], F32)
+        table_parts = table[:].rearrange("p g (s t h i) -> p g s t h i", s=2, t=PACK, h=2)
+        sin_turns = turns[:, 0].rearrange("p g (t i) -> p g t i", t=PACK)
+        cos_turns = turns[:, 1].rearrange("p g (t i) -> p g t i", t=PACK)
+
+        def fill_table():
+            nc.scalar.activation(out=table_parts[:, :, 0, :, 0, :], in_=cos_turns, func=SIN, scale=2.0 * math.pi)
+            nc.scalar.activation(out=table_parts[:, :, 0, :, 1, :], in_=cos_turns, func=SIN, scale=2.0 * math.pi)
+            nc.scalar.activation(out=table_parts[:, :, 1, :, 0, :], in_=sin_turns, func=SIN, scale=-2.0 * math.pi)
+            nc.scalar.activation(out=table_parts[:, :, 1, :, 1, :], in_=sin_turns, func=SIN, scale=2.0 * math.pi)
+
+        wd_grouped = consts.tile([P, OUT, PACK], BF16, align_bytes=64)
+        wd_codes = consts.tile([P, OUT], U32, align_bytes=64)
+        wd_scales = consts.tile([P, OUT], U8, align_bytes=64)
+
+        def regroup_wd():
+            views = []
+            for n in range(OUT_BANKS):
+                cols = slice(n * BANK, (n + 1) * BANK)
+                views.append(
+                    (
+                        wd_grouped[:, cols, :].rearrange("p (c i) t -> p c t i", i=4),
+                        wd_raw[:, :, cols].rearrange("p t (c i) -> p c t i", i=4),
+                    )
+                )
+            nc.scalar.copy(out=views[0][0], in_=views[0][1])
+            nc.vector.tensor_copy(out=views[1][0], in_=views[1][1])
+            nc.gpsimd.tensor_scalar(out=views[2][0], in0=views[2][1], scalar1=1.0, scalar2=0.0, op0=MULT, op1=ADD)
+
+        def quantise_wd():
+            for n in range(OUT_BANKS):
+                cols = slice(n * BANK, (n + 1) * BANK)
+                nc.vector.quantize_mx(
+                    out=wd_codes[:, cols].bitcast(FP8X4),
+                    scales=wd_scales[:, cols],
+                    in_=wd_grouped[:, cols, :].rearrange("p c t -> p (c t)"),
+                )
+
+        grouped_x, x_codes, x_scales, r_rows, products, grouped_r, r_codes, r_scales = {}, {}, {}, {}, {}, {}, {}, {}
+
+        def transpose_x(g, a):
+            if a == 0:
+                grouped_x[g] = work.tile([P, GROUP * PACK], BF16, align_bytes=64, name="grouped_x")
+            x_words = x_sb[g][:].bitcast(F32)
+            grouped_words = grouped_x[g][:].bitcast(F32).rearrange("q (a n u) -> q a n u", a=TILES, u=2)
+            xt = front_psum.tile([P, 2, P], F32, tag="front")
+            for u in range(2):
+                first = a * 2 * P + u
+                nc.tensor.transpose(xt[:, u, :], x_words[:, first : first + 2 * P - 1 : 2], ident_f32[:])
+            nc.scalar.copy(out=grouped_words[:, a], in_=xt[:].rearrange("q u n -> q n u"))
+
+        def quantise_x(g):
+            x_codes[g] = work.tile([P, GROUP], U32, align_bytes=64, name="x_codes")
+            x_scales[g] = work.tile([P, GROUP], U8, align_bytes=64, name="x_scales")
+            nc.vector.quantize_mx(out=x_codes[g][:].bitcast(FP8X4), scales=x_scales[g][:], in_=grouped_x[g][:])
+
+        def first_product(acc, g, a, cols):
+            tokens = slice(a * P, (a + 1) * P)
+            nc.tensor.matmul_mx(
+                out=acc,
+                lhsT=x_codes[g][:, tokens].bitcast(FP8X4),
+                lhsT_scale=x_scales[g][:, tokens],
+                rhs=wc_codes[:, cols].bitcast(FP8X4),
+                rhs_scale=wc_scales[:, cols],
+                start=True,
+                stop=True,
+            )
+
+        def paired_columns(g):
+            r_rows[g] = work.tile([P, TILES, PACK, P], BF16, name="r_rows")
+            paired = front_psum.tile([P, TILES, PAIRED], F32, tag="front")
+            for a in range(TILES):
+                first_product(paired[:, a, :], g, a, slice(DC, DC + PAIRED))
+            products[g] = work.tile([P, TILES, PAIRED], F32, name="products")
+            nc.vector.tensor_tensor(
+                out=products[g][:],
+                in0=paired[:],
+                in1=bc_cols[:, DC : DC + PAIRED, 0].unsqueeze(1).to_broadcast([P, TILES, PAIRED]),
+                op=ADD,
+            )
+
+        def rotate(g, engine):
+            h = g % GROUPS_PER_SEQUENCE
+            engine.tensor_tensor(
+                out=products[g][:], in0=products[g][:], in1=table[:, h * TILES : (h + 1) * TILES, :], op=MULT
+            )
+            engine.tensor_tensor(
+                out=r_rows[g][:, :, :, 0:ROT_P],
+                in0=products[g][:, :, 0:DR].rearrange("n a (t p) -> n a t p", t=PACK),
+                in1=products[g][:, :, DR:PAIRED].rearrange("n a (t p) -> n a t p", t=PACK),
+                op=ADD,
+            )
+
+        def other_columns(g, a):
+            c_acc = front_psum.tile([P, PACK, P], F32, tag="front")
+            first_product(c_acc[:].rearrange("n t p -> n (t p)"), g, a, slice(0, DC))
+            nc.vector.tensor_tensor(
+                out=r_rows[g][:, a, :, ROT_P:P],
+                in0=c_acc[:, :, ROT_P:P],
+                in1=bc_cols[:, 0:DC, 0].rearrange("n (t p) -> n t p", t=PACK)[:, :, ROT_P:P],
+                op=ADD,
+            )
+
+        def transpose_r(g, a):
+            if a == 0:
+                grouped_r[g] = work.tile([P, TILES, P, PACK], BF16, align_bytes=64, name="grouped_r")
+            rt = front_psum.tile([P, PACK, P], BF16, tag="front")
+            for t in range(PACK):
+                nc.tensor.transpose(rt[:, t, :], r_rows[g][:, a, t, :], ident_bf16[:])
+            nc.scalar.copy(out=grouped_r[g][:, a], in_=rt[:].rearrange("p t n -> p n t"))
+
+        def quantise_r(g):
+            r_codes[g] = work.tile([P, GROUP], U32, align_bytes=64, name="r_codes")
+            r_scales[g] = work.tile([P, GROUP], U8, align_bytes=64, name="r_scales")
+            nc.vector.quantize_mx(
+                out=r_codes[g][:].bitcast(FP8X4),
+                scales=r_scales[g][:],
+                in_=grouped_r[g][:].rearrange("p a n t -> p (a n t)"),
+            )
+
+        def second_product(g, a):
+            tokens = slice(a * P, (a + 1) * P)
+            result = results.tile([P, OUT], F32)
+            for n in range(OUT_BANKS):
+                cols = slice(n * BANK, (n + 1) * BANK)
+                acc = out_psum.tile([P, BANK], F32)
+                nc.tensor.matmul_mx(
+                    out=acc[:],
+                    lhsT=r_codes[g][:, tokens].bitcast(FP8X4),
+                    lhsT_scale=r_scales[g][:, tokens],
+                    rhs=wd_codes[:, cols].bitcast(FP8X4),
+                    rhs_scale=wd_scales[:, cols],
+                    start=True,
+                    stop=True,
+                )
+                if n == 0 or (n == 2 and (a < TWO_BANK_TILES or g + LAG_OUT - LAG_C >= GROUPS)):
+                    nc.vector.tensor_tensor(out=result[:, cols], in0=acc[:], in1=bd_all[:, cols], op=ADD)
+                else:
+                    nc.scalar.copy(out=result[:, cols], in_=acc[:])
+                    nc.gpsimd.tensor_tensor(out=result[:, cols], in0=result[:, cols], in1=bd_all[:, cols], op=ADD)
+            nc.sync.dma_start(out=out_groups[g][:, a, :], in_=result[:])
+
+        for step in range(GROUPS + LAG_OUT):
+            g_x, g_c, g_r, g_out = step, step - LAG_C, step - LAG_R, step - LAG_OUT
+            for a in range(TILES):
+                if 0 <= g_r < GROUPS:
+                    transpose_r(g_r, a)
+                if g_x < GROUPS:
+                    transpose_x(g_x, a)
+                if 0 <= g_c < GROUPS:
+                    if a == 0:
+                        paired_columns(g_c)
+                    other_columns(g_c, a)
+                if 0 <= g_out:
+                    second_product(g_out, a)
+            if step == 0:
+                fill_table()
+            if g_x < GROUPS:
+                quantise_x(g_x)
+            if step == LAG_C:
+                regroup_wd()
+            if 0 <= g_c < GROUPS:
+                rotate(g_c, nc.vector if 0 <= g_out else nc.gpsimd)
+            if step == LAG_C:
+                quantise_wd()
+            if 0 <= g_r < GROUPS:
+                quantise_r(g_r)

@@ -21,29 +21,23 @@ ROPE_BASE = 10000.0
 
 P = 128
 PACK = 4
+PAIR = 2
 TILES = 4
 GROUP = TILES * P
 GROUPS = B * S // GROUP
 GROUPS_PER_SEQUENCE = S // GROUP
+SLOT_TILES = 2
+SLOTS = GROUPS * TILES // SLOT_TILES
+POSITIONS = GROUPS_PER_SEQUENCE * TILES
 BANK = 512
 OUT_BANKS = OUT // BANK
 ROT_P = DR // PACK
+FAR = ROT_P // 2
+ROT_U = DR // 2
 PAIRED = 2 * DR
 ROUND_MAGIC = 1.5 * 2.0**23
-LAG_C, LAG_R, LAG_OUT = 1, 2, 3
-RESULT_BUFS = 2 * TILES
-TWO_BANK_TILES = 4
 
 FLOPS = 2 * B * S * D * DC + 2 * B * S * DC * OUT
-
-
-def append_partners(engine, cols):
-    slots = cols[:, 0:DC, :].rearrange("q (t p) w -> q t p w", t=PACK)
-    paired = cols[:, DC : DC + PAIRED, :].rearrange("q (s t p) w -> q s t p w", s=2, t=PACK)
-    far = ROT_P // 2
-    engine.tensor_copy(out=paired[:, 0], in_=slots[:, :, 0:ROT_P, :])
-    engine.tensor_copy(out=paired[:, 1, :, 0:far, :], in_=slots[:, :, far:ROT_P, :])
-    engine.tensor_copy(out=paired[:, 1, :, far:ROT_P, :], in_=slots[:, :, 0:far, :])
 
 
 def tile_deepseekmla_pa_t_kernel(tc, x, W_c, b_c, W_d, b_d, out):
@@ -54,243 +48,301 @@ def tile_deepseekmla_pa_t_kernel(tc, x, W_c, b_c, W_d, b_d, out):
     with ExitStack() as ctx:
         consts = ctx.enter_context(tc.tile_pool(name="consts", bufs=1))
         work = ctx.enter_context(tc.tile_pool(name="work", bufs=3))
-        results = ctx.enter_context(tc.tile_pool(name="results", bufs=RESULT_BUFS))
-        front_psum = ctx.enter_context(tc.psum_pool(name="front_psum", bufs=4))
+        results = ctx.enter_context(tc.tile_pool(name="results", bufs=10))
+        turn_psum = ctx.enter_context(tc.psum_pool(name="turn_psum", bufs=1))
+        c_psum = ctx.enter_context(tc.psum_pool(name="c_psum", bufs=2))
         out_psum = ctx.enter_context(tc.psum_pool(name="out_psum", bufs=4))
         ctx.enter_context(tc.manual_schedule())
 
         wc_raw = consts.tile([P, PACK, DC], BF16)
-        nc.sync.dma_start(
-            out=wc_raw[:],
-            in_=W_c.rearrange("(q k) c -> q k c", k=PACK),
-        )
+        nc.sync.dma_start(out=wc_raw[:], in_=W_c.rearrange("(q k) c -> q k c", k=PACK))
         x_sb = []
         for g in range(GROUPS):
             x_sb.append(consts.tile([P, TILES * D], BF16, name="x_sb%d" % g))
-        bc_raw = consts.tile([P, DC], BF16)
-        nc.sync.dma_start(out=bc_raw[:], in_=b_c.partition_broadcast(P))
-        for g in range(2):
-            nc.sync.dma_start(out=x_sb[g][:], in_=x_groups[g])
+        nc.sync.dma_start(out=x_sb[0][:, 0 : 2 * D], in_=x_groups[0][:, 0 : 2 * D])
+        nc.sync.dma_start(out=x_sb[0][:, 2 * D : 4 * D], in_=x_groups[0][:, 2 * D : 4 * D])
         wd_raw = consts.tile([P, PACK, OUT], BF16)
         wd_rows = W_d.rearrange("(p t) c -> p t c", t=PACK)
         for n in range(OUT_BANKS):
-            nc.sync.dma_start(
-                out=wd_raw[:, :, n * BANK : (n + 1) * BANK],
-                in_=wd_rows[:, :, n * BANK : (n + 1) * BANK],
-            )
-        bd_all = consts.tile([P, OUT], BF16)
-        nc.sync.dma_start(out=bd_all[:], in_=b_d.partition_broadcast(P))
-        for g in range(2, GROUPS):
+            cols = slice(n * BANK, (n + 1) * BANK)
+            nc.sync.dma_start(out=wd_raw[:, :, cols], in_=wd_rows[:, :, cols])
+        for g in range(1, GROUPS):
             nc.sync.dma_start(out=x_sb[g][:], in_=x_groups[g])
 
-        position = consts.tile([P, GROUPS_PER_SEQUENCE * TILES, 1], I32)
-        nc.gpsimd.iota(
-            position[:], pattern=[[GROUP, GROUPS_PER_SEQUENCE], [1, TILES]], base=0, channel_multiplier=TILES
-        )
-        ident_f32 = consts.tile([P, P], F32)
-        make_identity(nc, ident_f32[:])
-        ident_bf16 = consts.tile([P, P], BF16)
-        make_identity(nc, ident_bf16[:])
-        turns = consts.tile([P, 2, GROUPS_PER_SEQUENCE * TILES, HALF], F32)
-        for j in range(HALF):
-            column = (j % PACK) * (HALF // PACK) + j // PACK
+        ones = consts.tile([P, P], BF16)
+        bias_rows = []
+        for n in range(1 + OUT_BANKS):
+            bias_rows.append(consts.tile([P, BANK], BF16, name="bias_rows%d" % n))
+        nc.vector.memset(bias_rows[0][:].bitcast(I32), 0)
+        nc.vector.memset(ones[:], 1.0)
+        nc.scalar.dma_start(out=bias_rows[0][0:1, :], in_=b_c.unsqueeze(0))
+        position = consts.tile([P, POSITIONS, 1], I32)
+        nc.gpsimd.iota(position[:], pattern=[[GROUP, GROUPS_PER_SEQUENCE], [1, TILES]], base=0, channel_multiplier=TILES)
+        ident = consts.tile([P, P], F32)
+        make_identity(nc, ident[:])
+        for n in range(OUT_BANKS):
+            nc.gpsimd.memset(bias_rows[1 + n][:].bitcast(I32), 0)
+            nc.scalar.dma_start(out=bias_rows[1 + n][0:1, :], in_=b_d.unsqueeze(0)[:, n * BANK : (n + 1) * BANK])
+        warm = consts.tile([P, 1], F32)
+        nc.vector.memset(warm[:], 0.0)
+        nc.scalar.activation(out=warm[:], in_=warm[:], func=SIN)
+        turns = consts.tile([P, 2, POSITIONS, HALF], F32)
+        for j in range(2 * PACK):
+            column = 16 * (j // 2 % 2) + 2 * (j // 4) + j % 2
             nc.vector.tensor_scalar_mul(
                 out=turns[:, 0, :, column : column + 1],
                 in0=position[:],
                 scalar1=1.0 / ROPE_BASE ** (2.0 * j / DR) / (2.0 * math.pi),
             )
-
-        wc_grouped = consts.tile([P, DC + PAIRED, PACK], BF16, align_bytes=64)
-        nc.vector.tensor_copy(
-            out=wc_grouped[:, 0:DC, :].rearrange("q (t p) k -> q t p k", t=PACK),
-            in_=wc_raw[:].rearrange("q k (p t) -> q t p k", t=PACK),
-        )
-        append_partners(nc.vector, wc_grouped[:])
-        wc_codes = consts.tile([P, DC + PAIRED], U32, align_bytes=64)
-        wc_scales = consts.tile([P, DC + PAIRED], U8, align_bytes=64)
-        for cols in (slice(0, DC), slice(DC, DC + PAIRED)):
-            nc.vector.quantize_mx(
-                out=wc_codes[:, cols].bitcast(FP8X4),
-                scales=wc_scales[:, cols],
-                in_=wc_grouped[:, cols, :].rearrange("q c k -> q (c k)"),
+        by_i = turns[:, 0].rearrange("p g (u c) -> p (g u) c", u=2)
+        for i in (2, 4):
+            nc.vector.tensor_scalar_mul(
+                out=by_i[:, :, PAIR * i : 2 * PAIR * i],
+                in0=by_i[:, :, 0 : PAIR * i],
+                scalar1=1.0 / ROPE_BASE ** (2.0 * PACK * i / DR),
             )
-        bc_cols = consts.tile([P, DC + PAIRED, 1], F32)
-        nc.gpsimd.tensor_copy(
-            out=bc_cols[:, 0:DC, 0].rearrange("q (t p) -> q t p", t=PACK),
-            in_=bc_raw[:].rearrange("q (p t) -> q t p", t=PACK),
-        )
-        append_partners(nc.gpsimd, bc_cols[:])
-
         nc.vector.tensor_scalar_add(out=turns[:, 1], in0=turns[:, 0], scalar1=0.25)
-        whole = consts.tile([P, 2, GROUPS_PER_SEQUENCE * TILES, HALF], F32)
+        whole = consts.tile([P, 2, POSITIONS, HALF], F32)
         nc.vector.tensor_scalar(
             out=whole[:], in0=turns[:], scalar1=ROUND_MAGIC, scalar2=ROUND_MAGIC, op0=ADD, op1=SUBTRACT
         )
         nc.vector.tensor_tensor(out=turns[:], in0=turns[:], in1=whole[:], op=SUBTRACT)
-        table = consts.tile([P, GROUPS_PER_SEQUENCE * TILES, PAIRED], F32)
-        table_parts = table[:].rearrange("p g (s t h i) -> p g s t h i", s=2, t=PACK, h=2)
-        sin_turns = turns[:, 0].rearrange("p g (t i) -> p g t i", t=PACK)
-        cos_turns = turns[:, 1].rearrange("p g (t i) -> p g t i", t=PACK)
+        table = consts.tile([P, 2, POSITIONS, DR], F32)
 
         def fill_table():
-            nc.scalar.activation(out=table_parts[:, :, 0, :, 0, :], in_=cos_turns, func=SIN, scale=2.0 * math.pi)
-            nc.scalar.activation(out=table_parts[:, :, 0, :, 1, :], in_=cos_turns, func=SIN, scale=2.0 * math.pi)
-            nc.scalar.activation(out=table_parts[:, :, 1, :, 0, :], in_=sin_turns, func=SIN, scale=-2.0 * math.pi)
-            nc.scalar.activation(out=table_parts[:, :, 1, :, 1, :], in_=sin_turns, func=SIN, scale=2.0 * math.pi)
+            turn = 2.0 * math.pi
+            for s, far, scale in ((0, 0, turn), (0, 1, turn), (1, 0, -turn), (1, 1, turn)):
+                nc.scalar.activation(
+                    out=table[:, s].rearrange("p g (u h i) -> p (g u) h i", u=2, h=2)[:, :, far, :],
+                    in_=turns[:, 1 - s].rearrange("p g (u i) -> p (g u) i", u=2),
+                    func=SIN,
+                    scale=scale,
+                )
+
+        wc_grouped = consts.tile([P, DC + PAIRED, PACK], BF16, align_bytes=64)
+        wc_codes = consts.tile([P, DC + PAIRED], U32, align_bytes=64)
+        wc_scales = consts.tile([P, DC + PAIRED], U8, align_bytes=64)
+        bc_cols = consts.tile([P, DC + PAIRED, 1], F32)
+        bd_all = consts.tile([P, OUT], BF16)
+
+        def spread_bias(i):
+            acc = out_psum.tile([P, BANK], F32, tag="out")
+            nc.tensor.matmul(acc[:], lhsT=ones[:], rhs=bias_rows[i][:], start=True, stop=True)
+            if i == 0:
+                for u in range(2):
+                    nc.scalar.copy(
+                        out=bc_cols[:, u * 256 : (u + 1) * 256, 0].rearrange("n (p e) -> n p e", e=PAIR),
+                        in_=acc[:].rearrange("n (p u e) -> n u p e", u=2, e=PAIR)[:, u],
+                    )
+            else:
+                nc.scalar.copy(out=bd_all[:, (i - 1) * BANK : i * BANK], in_=acc[:])
+
+        def append_partners(engine, cols):
+            halves = cols[:, 0:DC, :].rearrange("q (u c) w -> q u (c w)", u=2)
+            paired = cols[:, DC : DC + PAIRED, :].rearrange("q (s u c) w -> q s u (c w)", s=2, u=2)
+            mid = halves.shape[2] // 256 * PAIR * FAR
+            end = 2 * mid
+            engine.tensor_copy(out=paired[:, 0], in_=halves[:, :, 0:end])
+            engine.tensor_copy(out=paired[:, 1, :, 0:mid], in_=halves[:, :, mid:end])
+            engine.tensor_copy(out=paired[:, 1, :, mid:end], in_=halves[:, :, 0:mid])
 
         wd_grouped = consts.tile([P, OUT, PACK], BF16, align_bytes=64)
         wd_codes = consts.tile([P, OUT], U32, align_bytes=64)
         wd_scales = consts.tile([P, OUT], U8, align_bytes=64)
 
-        def regroup_wd():
-            views = []
-            for n in range(OUT_BANKS):
-                cols = slice(n * BANK, (n + 1) * BANK)
-                views.append(
-                    (
-                        wd_grouped[:, cols, :].rearrange("p (c i) t -> p c t i", i=4),
-                        wd_raw[:, :, cols].rearrange("p t (c i) -> p c t i", i=4),
-                    )
-                )
-            nc.scalar.copy(out=views[0][0], in_=views[0][1])
-            nc.vector.tensor_copy(out=views[1][0], in_=views[1][1])
-            nc.gpsimd.tensor_scalar(out=views[2][0], in0=views[2][1], scalar1=1.0, scalar2=0.0, op0=MULT, op1=ADD)
+        def regroup_wd(n):
+            cols = slice(n * BANK, (n + 1) * BANK)
+            wide = wd_grouped[:, cols, :].rearrange("p (c i) t -> p c t i", i=4)
+            rows = wd_raw[:, :, cols].rearrange("p t (c i) -> p c t i", i=4)
+            if n == 2:
+                nc.scalar.copy(out=wide, in_=rows)
+            else:
+                nc.vector.tensor_copy(out=wide, in_=rows)
 
-        def quantise_wd():
-            for n in range(OUT_BANKS):
-                cols = slice(n * BANK, (n + 1) * BANK)
-                nc.vector.quantize_mx(
-                    out=wd_codes[:, cols].bitcast(FP8X4),
-                    scales=wd_scales[:, cols],
-                    in_=wd_grouped[:, cols, :].rearrange("p c t -> p (c t)"),
-                )
+        def quantise_wd(n):
+            cols = slice(n * BANK, (n + 1) * BANK)
+            nc.vector.quantize_mx(
+                out=wd_codes[:, cols].bitcast(FP8X4),
+                scales=wd_scales[:, cols],
+                in_=wd_grouped[:, cols, :].rearrange("p c t -> p (c t)"),
+            )
 
         grouped_x, x_codes, x_scales, r_rows, products, grouped_r, r_codes, r_scales = {}, {}, {}, {}, {}, {}, {}, {}
 
-        def transpose_x(g, a):
-            if a == 0:
-                grouped_x[g] = work.tile([P, GROUP * PACK], BF16, align_bytes=64, name="grouped_x")
-            x_words = x_sb[g][:].bitcast(F32)
-            grouped_words = grouped_x[g][:].bitcast(F32).rearrange("q (a n u) -> q a n u", a=TILES, u=2)
-            xt = front_psum.tile([P, 2, P], F32, tag="front")
-            for u in range(2):
-                first = a * 2 * P + u
-                nc.tensor.transpose(xt[:, u, :], x_words[:, first : first + 2 * P - 1 : 2], ident_f32[:])
-            nc.scalar.copy(out=grouped_words[:, a], in_=xt[:].rearrange("q u n -> q n u"))
+        def transpose_x(k):
+            grouped_x[k] = work.tile([P, SLOT_TILES * P * PACK], BF16, align_bytes=64, name="grouped_x")
+            words = x_sb[k // 2][:].bitcast(F32)
+            xt = turn_psum.tile([P, SLOT_TILES, 2, P], F32, tag="xt")
+            for a in range(SLOT_TILES):
+                for u in range(2):
+                    first = (k % 2 * SLOT_TILES + a) * 2 * P + u
+                    nc.tensor.transpose(xt[:, a, u, :], words[:, first : first + 2 * P - 1 : 2], ident[:])
+            nc.scalar.copy(
+                out=grouped_x[k][:].bitcast(F32).rearrange("q (a n u) -> q a n u", a=SLOT_TILES, u=2),
+                in_=xt[:].rearrange("q a u n -> q a n u"),
+            )
 
-        def quantise_x(g):
-            x_codes[g] = work.tile([P, GROUP], U32, align_bytes=64, name="x_codes")
-            x_scales[g] = work.tile([P, GROUP], U8, align_bytes=64, name="x_scales")
-            nc.vector.quantize_mx(out=x_codes[g][:].bitcast(FP8X4), scales=x_scales[g][:], in_=grouped_x[g][:])
+        def quantise(codes, scales, grouped, k, name):
+            codes[k] = work.tile([P, SLOT_TILES * P], U32, align_bytes=64, name=name + "_codes")
+            scales[k] = work.tile([P, SLOT_TILES * P], U8, align_bytes=64, name=name + "_scales")
+            nc.vector.quantize_mx(out=codes[k][:].bitcast(FP8X4), scales=scales[k][:], in_=grouped[k][:])
 
-        def first_product(acc, g, a, cols):
+        def first_product(acc, k, a, cols):
             tokens = slice(a * P, (a + 1) * P)
             nc.tensor.matmul_mx(
                 out=acc,
-                lhsT=x_codes[g][:, tokens].bitcast(FP8X4),
-                lhsT_scale=x_scales[g][:, tokens],
+                lhsT=x_codes[k][:, tokens].bitcast(FP8X4),
+                lhsT_scale=x_scales[k][:, tokens],
                 rhs=wc_codes[:, cols].bitcast(FP8X4),
                 rhs_scale=wc_scales[:, cols],
                 start=True,
                 stop=True,
             )
 
-        def paired_columns(g):
-            r_rows[g] = work.tile([P, TILES, PACK, P], BF16, name="r_rows")
-            paired = front_psum.tile([P, TILES, PAIRED], F32, tag="front")
-            for a in range(TILES):
-                first_product(paired[:, a, :], g, a, slice(DC, DC + PAIRED))
-            products[g] = work.tile([P, TILES, PAIRED], F32, name="products")
+        def paired_columns(k):
+            at = k * SLOT_TILES % POSITIONS
+            r_rows[k] = work.tile([P, SLOT_TILES, 2, 256], BF16, name="r_rows")
+            paired = c_psum.tile([P, SLOT_TILES, 2, DR], F32, tag="c")
+            for a in range(SLOT_TILES):
+                first_product(paired[:, a].rearrange("n s c -> n (s c)"), k, a, slice(DC, DC + PAIRED))
+            products[k] = work.tile([P, SLOT_TILES, 2, DR], F32, name="products")
             nc.vector.tensor_tensor(
-                out=products[g][:],
+                out=products[k][:],
                 in0=paired[:],
-                in1=bc_cols[:, DC : DC + PAIRED, 0].unsqueeze(1).to_broadcast([P, TILES, PAIRED]),
+                in1=table[:, :, at : at + SLOT_TILES, :].rearrange("n s a c -> n a s c"),
+                op=MULT,
+            )
+
+        def rotate(k):
+            at = k * SLOT_TILES % POSITIONS
+            nc.gpsimd.tensor_tensor(
+                out=products[k][:, :, 0, :], in0=products[k][:, :, 0, :], in1=products[k][:, :, 1, :], op=ADD
+            )
+            nc.gpsimd.tensor_tensor(
+                out=r_rows[k][:, :, :, 0:ROT_U],
+                in0=products[k][:, :, 0, :].rearrange("n a (u c) -> n a u c", u=2),
+                in1=rotated_bias[:, at : at + SLOT_TILES, :].rearrange("n a (u c) -> n a u c", u=2),
                 op=ADD,
             )
 
-        def rotate(g, engine):
-            h = g % GROUPS_PER_SEQUENCE
-            engine.tensor_tensor(
-                out=products[g][:], in0=products[g][:], in1=table[:, h * TILES : (h + 1) * TILES, :], op=MULT
-            )
-            engine.tensor_tensor(
-                out=r_rows[g][:, :, :, 0:ROT_P],
-                in0=products[g][:, :, 0:DR].rearrange("n a (t p) -> n a t p", t=PACK),
-                in1=products[g][:, :, DR:PAIRED].rearrange("n a (t p) -> n a t p", t=PACK),
-                op=ADD,
-            )
-
-        def other_columns(g, a):
-            c_acc = front_psum.tile([P, PACK, P], F32, tag="front")
-            first_product(c_acc[:].rearrange("n t p -> n (t p)"), g, a, slice(0, DC))
+        def other_columns(k, a):
+            c_acc = c_psum.tile([P, 2, 256], F32, tag="c")
+            first_product(c_acc[:].rearrange("n u c -> n (u c)"), k, a, slice(0, DC))
             nc.vector.tensor_tensor(
-                out=r_rows[g][:, a, :, ROT_P:P],
-                in0=c_acc[:, :, ROT_P:P],
-                in1=bc_cols[:, 0:DC, 0].rearrange("n (t p) -> n t p", t=PACK)[:, :, ROT_P:P],
+                out=r_rows[k][:, a, :, ROT_U:256],
+                in0=c_acc[:, :, ROT_U:256],
+                in1=bc_cols[:, 0:DC, 0].rearrange("n (u c) -> n u c", u=2)[:, :, ROT_U:256],
                 op=ADD,
             )
 
-        def transpose_r(g, a):
-            if a == 0:
-                grouped_r[g] = work.tile([P, TILES, P, PACK], BF16, align_bytes=64, name="grouped_r")
-            rt = front_psum.tile([P, PACK, P], BF16, tag="front")
-            for t in range(PACK):
-                nc.tensor.transpose(rt[:, t, :], r_rows[g][:, a, t, :], ident_bf16[:])
-            nc.scalar.copy(out=grouped_r[g][:, a], in_=rt[:].rearrange("p t n -> p n t"))
-
-        def quantise_r(g):
-            r_codes[g] = work.tile([P, GROUP], U32, align_bytes=64, name="r_codes")
-            r_scales[g] = work.tile([P, GROUP], U8, align_bytes=64, name="r_scales")
-            nc.vector.quantize_mx(
-                out=r_codes[g][:].bitcast(FP8X4),
-                scales=r_scales[g][:],
-                in_=grouped_r[g][:].rearrange("p a n t -> p (a n t)"),
+        def transpose_r(k):
+            grouped_r[k] = work.tile([P, SLOT_TILES * P * PACK], BF16, align_bytes=64, name="grouped_r")
+            words = r_rows[k][:].rearrange("n a u c -> n (a u c)").bitcast(F32)
+            rt = turn_psum.tile([P, SLOT_TILES, 2, P], F32, tag="rt")
+            for a in range(SLOT_TILES):
+                for u in range(2):
+                    first = (a * 2 + u) * P
+                    nc.tensor.transpose(rt[:, a, u, :], words[:, first : first + P], ident[:])
+            nc.scalar.copy(
+                out=grouped_r[k][:].bitcast(F32).rearrange("p (a n u) -> p a n u", a=SLOT_TILES, u=2),
+                in_=rt[:].rearrange("p a u n -> p a n u"),
             )
 
-        def second_product(g, a):
+        def second_product(k, a, n, on_vector, result):
             tokens = slice(a * P, (a + 1) * P)
-            result = results.tile([P, OUT], F32)
-            for n in range(OUT_BANKS):
-                cols = slice(n * BANK, (n + 1) * BANK)
-                acc = out_psum.tile([P, BANK], F32)
-                nc.tensor.matmul_mx(
-                    out=acc[:],
-                    lhsT=r_codes[g][:, tokens].bitcast(FP8X4),
-                    lhsT_scale=r_scales[g][:, tokens],
-                    rhs=wd_codes[:, cols].bitcast(FP8X4),
-                    rhs_scale=wd_scales[:, cols],
-                    start=True,
-                    stop=True,
-                )
-                if n == 0 or (n == 2 and (a < TWO_BANK_TILES or g + LAG_OUT - LAG_C >= GROUPS)):
-                    nc.vector.tensor_tensor(out=result[:, cols], in0=acc[:], in1=bd_all[:, cols], op=ADD)
-                else:
-                    nc.scalar.copy(out=result[:, cols], in_=acc[:])
-                    nc.gpsimd.tensor_tensor(out=result[:, cols], in0=result[:, cols], in1=bd_all[:, cols], op=ADD)
-            nc.sync.dma_start(out=out_groups[g][:, a, :], in_=result[:])
+            cols = slice(n * BANK, (n + 1) * BANK)
+            acc = out_psum.tile([P, BANK], F32, tag="out")
+            nc.tensor.matmul_mx(
+                out=acc[:],
+                lhsT=r_codes[k][:, tokens].bitcast(FP8X4),
+                lhsT_scale=r_scales[k][:, tokens],
+                rhs=wd_codes[:, cols].bitcast(FP8X4),
+                rhs_scale=wd_scales[:, cols],
+                start=True,
+                stop=True,
+            )
+            if on_vector:
+                nc.vector.tensor_tensor(out=result[:, cols], in0=acc[:], in1=bd_all[:, cols], op=ADD)
+            else:
+                nc.scalar.copy(out=result[:, cols], in_=acc[:])
+                nc.gpsimd.tensor_tensor(out=result[:, cols], in0=result[:, cols], in1=bd_all[:, cols], op=ADD)
 
-        for step in range(GROUPS + LAG_OUT):
-            g_x, g_c, g_r, g_out = step, step - LAG_C, step - LAG_R, step - LAG_OUT
-            for a in range(TILES):
-                if 0 <= g_r < GROUPS:
-                    transpose_r(g_r, a)
-                if g_x < GROUPS:
-                    transpose_x(g_x, a)
-                if 0 <= g_c < GROUPS:
-                    if a == 0:
-                        paired_columns(g_c)
-                    other_columns(g_c, a)
-                if 0 <= g_out:
-                    second_product(g_out, a)
-            if step == 0:
+        for u in range(2):
+            latent = wc_grouped[:, u * 256 : (u + 1) * 256, :].rearrange("q (p e) k -> q p k e", e=PAIR)
+            rows = wc_raw[:].rearrange("q k (p u e) -> q u p k e", u=2, e=PAIR)[:, u]
+            if u == 0:
+                nc.vector.tensor_copy(out=latent, in_=rows)
+            else:
+                nc.scalar.copy(out=latent, in_=rows)
+        append_partners(nc.vector, wc_grouped[:])
+        for cols in (slice(DC, DC + PAIRED), slice(0, DC)):
+            nc.vector.quantize_mx(
+                out=wc_codes[:, cols].bitcast(FP8X4),
+                scales=wc_scales[:, cols],
+                in_=wc_grouped[:, cols, :].rearrange("q c k -> q (c k)"),
+            )
+        rotated_bias = consts.tile([P, POSITIONS, DR], F32)
+        bias_part = consts.tile([P, POSITIONS, DR], F32)
+
+        def rotate_bias(h):
+            at = slice(h * TILES, (h + 1) * TILES)
+            for s, into in ((0, rotated_bias), (1, bias_part)):
+                pair_bias = bc_cols[:, DC + s * DR : DC + (s + 1) * DR, 0]
+                nc.gpsimd.tensor_tensor(
+                    out=into[:, at],
+                    in0=table[:, s, at],
+                    in1=pair_bias.unsqueeze(1).to_broadcast([P, TILES, DR]),
+                    op=MULT,
+                )
+            nc.gpsimd.tensor_tensor(out=rotated_bias[:, at], in0=rotated_bias[:, at], in1=bias_part[:, at], op=ADD)
+
+        for k in range(SLOTS + 3):
+            k_c, k_r, k_out = k - 1, k - 2, k - 3
+            has_c, has_r, has_out = 0 <= k_c < SLOTS, 0 <= k_r < SLOTS, 0 <= k_out
+            if k < SLOTS:
+                transpose_x(k)
+            if k == 0:
+                spread_bias(0)
+                append_partners(nc.gpsimd, bc_cols[:])
                 fill_table()
-            if g_x < GROUPS:
-                quantise_x(g_x)
-            if step == LAG_C:
-                regroup_wd()
-            if 0 <= g_c < GROUPS:
-                rotate(g_c, nc.vector if 0 <= g_out else nc.gpsimd)
-            if step == LAG_C:
-                quantise_wd()
-            if 0 <= g_r < GROUPS:
-                quantise_r(g_r)
+                rotate_bias(0)
+            if has_r:
+                transpose_r(k_r)
+            if has_c:
+                paired_columns(k_c)
+                rotate(k_c)
+            vector_work = []
+            if k < SLOTS:
+                vector_work.append(lambda: quantise(x_codes, x_scales, grouped_x, k, "x"))
+            if has_r:
+                vector_work.append(lambda: quantise(r_codes, r_scales, grouped_r, k_r, "r"))
+            tail = k_out >= SLOTS - 2
+            banks = []
+            if has_out:
+                for a in range(SLOT_TILES):
+                    result = results.tile([P, OUT], F32, name="result")
+                    for n in (1, 0, 2):
+                        on_vector = n == 0 or (n == 2 and (tail or (k_out * SLOT_TILES + a) % 4 != 3))
+                        banks.append((a, n, on_vector, result))
+            for i in range(max(len(banks), SLOT_TILES)):
+                if has_c and i < SLOT_TILES:
+                    other_columns(k_c, i)
+                if i < len(banks):
+                    a, n, on_vector, result = banks[i]
+                    second_product(k_out, a, n, on_vector, result)
+                    if n == 2:
+                        tile_of_group = k_out % 2 * SLOT_TILES + a
+                        nc.sync.dma_start(out=out_groups[k_out // 2][:, tile_of_group, :], in_=result[:])
+                if i >= 1 and vector_work:
+                    vector_work.pop(0)()
+            for job in vector_work:
+                job()
+            if k == 1:
+                rotate_bias(1)
+                for n in (1, 0, 2):
+                    regroup_wd(n)
+            if k == 2:
+                for n in range(OUT_BANKS):
+                    spread_bias(1 + n)
+                for n in (1, 0, 2):
+                    quantise_wd(n)

@@ -54,6 +54,11 @@ def tile_deepseekmla_pa_t_kernel(tc, x, W_c, b_c, W_d, b_d, out):
         out_psum = ctx.enter_context(tc.psum_pool(name="out_psum", bufs=4))
         ctx.enter_context(tc.manual_schedule())
 
+        bc_rows = consts.tile([P, DC], BF16)
+        nc.vector.memset(bc_rows[:].bitcast(I32), 0)
+        nc.sync.dma_start(out=bc_rows[0:1, :], in_=b_c.unsqueeze(0))
+        bd_rows = consts.tile([P, OUT], BF16)
+        nc.gpsimd.memset(bd_rows[:].bitcast(I32), 0)
         wc_raw = consts.tile([P, PACK, DC], BF16)
         nc.sync.dma_start(out=wc_raw[:], in_=W_c.rearrange("(q k) c -> q k c", k=PACK))
         x_sb = []
@@ -66,26 +71,19 @@ def tile_deepseekmla_pa_t_kernel(tc, x, W_c, b_c, W_d, b_d, out):
         for n in range(OUT_BANKS):
             cols = slice(n * BANK, (n + 1) * BANK)
             nc.sync.dma_start(out=wd_raw[:, :, cols], in_=wd_rows[:, :, cols])
+        nc.sync.dma_start(out=bd_rows[0:1, :], in_=b_d.unsqueeze(0))
         for g in range(1, GROUPS):
             nc.sync.dma_start(out=x_sb[g][:], in_=x_groups[g])
 
         ones = consts.tile([P, P], BF16)
-        bias_rows = []
-        for n in range(1 + OUT_BANKS):
-            bias_rows.append(consts.tile([P, BANK], BF16, name="bias_rows%d" % n))
-        nc.vector.memset(bias_rows[0][:].bitcast(I32), 0)
         nc.vector.memset(ones[:], 1.0)
-        nc.scalar.dma_start(out=bias_rows[0][0:1, :], in_=b_c.unsqueeze(0))
+        warm = consts.tile([P, 1], F32)
+        nc.vector.memset(warm[:], 0.0)
+        nc.scalar.activation(out=warm[:], in_=warm[:], func=SIN)
         position = consts.tile([P, POSITIONS, 1], I32)
         nc.gpsimd.iota(position[:], pattern=[[GROUP, GROUPS_PER_SEQUENCE], [1, TILES]], base=0, channel_multiplier=TILES)
         ident = consts.tile([P, P], F32)
         make_identity(nc, ident[:])
-        for n in range(OUT_BANKS):
-            nc.gpsimd.memset(bias_rows[1 + n][:].bitcast(I32), 0)
-            nc.scalar.dma_start(out=bias_rows[1 + n][0:1, :], in_=b_d.unsqueeze(0)[:, n * BANK : (n + 1) * BANK])
-        warm = consts.tile([P, 1], F32)
-        nc.vector.memset(warm[:], 0.0)
-        nc.scalar.activation(out=warm[:], in_=warm[:], func=SIN)
         turns = consts.tile([P, 2, POSITIONS, HALF], F32)
         for j in range(2 * PACK):
             column = 16 * (j // 2 % 2) + 2 * (j // 4) + j % 2
@@ -125,17 +123,20 @@ def tile_deepseekmla_pa_t_kernel(tc, x, W_c, b_c, W_d, b_d, out):
         bc_cols = consts.tile([P, DC + PAIRED, 1], F32)
         bd_all = consts.tile([P, OUT], BF16)
 
-        def spread_bias(i):
+        def spread_bc():
             acc = out_psum.tile([P, BANK], F32, tag="out")
-            nc.tensor.matmul(acc[:], lhsT=ones[:], rhs=bias_rows[i][:], start=True, stop=True)
-            if i == 0:
-                for u in range(2):
-                    nc.scalar.copy(
-                        out=bc_cols[:, u * 256 : (u + 1) * 256, 0].rearrange("n (p e) -> n p e", e=PAIR),
-                        in_=acc[:].rearrange("n (p u e) -> n u p e", u=2, e=PAIR)[:, u],
-                    )
-            else:
-                nc.scalar.copy(out=bd_all[:, (i - 1) * BANK : i * BANK], in_=acc[:])
+            nc.tensor.matmul(acc[:], lhsT=ones[:], rhs=bc_rows[:], start=True, stop=True)
+            for u in range(2):
+                nc.scalar.copy(
+                    out=bc_cols[:, u * 256 : (u + 1) * 256, 0].rearrange("n (p e) -> n p e", e=PAIR),
+                    in_=acc[:].rearrange("n (p u e) -> n u p e", u=2, e=PAIR)[:, u],
+                )
+
+        def spread_bd(n):
+            cols = slice(n * BANK, (n + 1) * BANK)
+            acc = out_psum.tile([P, BANK], F32, tag="out")
+            nc.tensor.matmul(acc[:], lhsT=ones[:], rhs=bd_rows[:, cols], start=True, stop=True)
+            nc.scalar.copy(out=bd_all[:, cols], in_=acc[:])
 
         def append_partners(engine, cols):
             halves = cols[:, 0:DC, :].rearrange("q (u c) w -> q u (c w)", u=2)
@@ -167,10 +168,10 @@ def tile_deepseekmla_pa_t_kernel(tc, x, W_c, b_c, W_d, b_d, out):
                 in_=wd_grouped[:, cols, :].rearrange("p c t -> p (c t)"),
             )
 
-        grouped_x, x_codes, x_scales, r_rows, products, grouped_r, r_codes, r_scales = {}, {}, {}, {}, {}, {}, {}, {}
+        SPAN = SLOT_TILES * P
+        grouped, codes, scales, r_rows, products = {}, {}, {}, {}, {}
 
         def transpose_x(k):
-            grouped_x[k] = work.tile([P, SLOT_TILES * P * PACK], BF16, align_bytes=64, name="grouped_x")
             words = x_sb[k // 2][:].bitcast(F32)
             xt = turn_psum.tile([P, SLOT_TILES, 2, P], F32, tag="xt")
             for a in range(SLOT_TILES):
@@ -178,21 +179,26 @@ def tile_deepseekmla_pa_t_kernel(tc, x, W_c, b_c, W_d, b_d, out):
                     first = (k % 2 * SLOT_TILES + a) * 2 * P + u
                     nc.tensor.transpose(xt[:, a, u, :], words[:, first : first + 2 * P - 1 : 2], ident[:])
             nc.scalar.copy(
-                out=grouped_x[k][:].bitcast(F32).rearrange("q (a n u) -> q a n u", a=SLOT_TILES, u=2),
+                out=grouped[k][:, 0].bitcast(F32).rearrange("q (a n u) -> q a n u", a=SLOT_TILES, u=2),
                 in_=xt[:].rearrange("q a u n -> q a n u"),
             )
 
-        def quantise(codes, scales, grouped, k, name):
-            codes[k] = work.tile([P, SLOT_TILES * P], U32, align_bytes=64, name=name + "_codes")
-            scales[k] = work.tile([P, SLOT_TILES * P], U8, align_bytes=64, name=name + "_scales")
-            nc.vector.quantize_mx(out=codes[k][:].bitcast(FP8X4), scales=scales[k][:], in_=grouped[k][:])
+        def quantise(k):
+            parts = slice(0 if k < SLOTS else 1, 2 if k >= 2 else 1)
+            codes[k] = work.tile([P, 2, SPAN], U32, align_bytes=64, name="codes")
+            scales[k] = work.tile([P, 2, SPAN], U8, align_bytes=64, name="scales")
+            nc.vector.quantize_mx(
+                out=codes[k][:, parts].rearrange("p s n -> p (s n)").bitcast(FP8X4),
+                scales=scales[k][:, parts].rearrange("p s n -> p (s n)"),
+                in_=grouped[k][:, parts].rearrange("p s n -> p (s n)"),
+            )
 
         def first_product(acc, k, a, cols):
             tokens = slice(a * P, (a + 1) * P)
             nc.tensor.matmul_mx(
                 out=acc,
-                lhsT=x_codes[k][:, tokens].bitcast(FP8X4),
-                lhsT_scale=x_scales[k][:, tokens],
+                lhsT=codes[k][:, 0, tokens].bitcast(FP8X4),
+                lhsT_scale=scales[k][:, 0, tokens],
                 rhs=wc_codes[:, cols].bitcast(FP8X4),
                 rhs_scale=wc_scales[:, cols],
                 start=True,
@@ -236,7 +242,6 @@ def tile_deepseekmla_pa_t_kernel(tc, x, W_c, b_c, W_d, b_d, out):
             )
 
         def transpose_r(k):
-            grouped_r[k] = work.tile([P, SLOT_TILES * P * PACK], BF16, align_bytes=64, name="grouped_r")
             words = r_rows[k][:].rearrange("n a u c -> n (a u c)").bitcast(F32)
             rt = turn_psum.tile([P, SLOT_TILES, 2, P], F32, tag="rt")
             for a in range(SLOT_TILES):
@@ -244,7 +249,7 @@ def tile_deepseekmla_pa_t_kernel(tc, x, W_c, b_c, W_d, b_d, out):
                     first = (a * 2 + u) * P
                     nc.tensor.transpose(rt[:, a, u, :], words[:, first : first + P], ident[:])
             nc.scalar.copy(
-                out=grouped_r[k][:].bitcast(F32).rearrange("p (a n u) -> p a n u", a=SLOT_TILES, u=2),
+                out=grouped[k + 2][:, 1].bitcast(F32).rearrange("p (a n u) -> p a n u", a=SLOT_TILES, u=2),
                 in_=rt[:].rearrange("p a u n -> p a n u"),
             )
 
@@ -254,8 +259,8 @@ def tile_deepseekmla_pa_t_kernel(tc, x, W_c, b_c, W_d, b_d, out):
             acc = out_psum.tile([P, BANK], F32, tag="out")
             nc.tensor.matmul_mx(
                 out=acc[:],
-                lhsT=r_codes[k][:, tokens].bitcast(FP8X4),
-                lhsT_scale=r_scales[k][:, tokens],
+                lhsT=codes[k + 2][:, 1, tokens].bitcast(FP8X4),
+                lhsT_scale=scales[k + 2][:, 1, tokens],
                 rhs=wd_codes[:, cols].bitcast(FP8X4),
                 rhs_scale=wd_scales[:, cols],
                 start=True,
@@ -265,8 +270,12 @@ def tile_deepseekmla_pa_t_kernel(tc, x, W_c, b_c, W_d, b_d, out):
                 nc.vector.tensor_tensor(out=result[:, cols], in0=acc[:], in1=bd_all[:, cols], op=ADD)
             else:
                 nc.scalar.copy(out=result[:, cols], in_=acc[:])
-                nc.gpsimd.tensor_tensor(out=result[:, cols], in0=result[:, cols], in1=bd_all[:, cols], op=ADD)
+                for half in range(2):
+                    part = slice(n * BANK + half * BANK // 2, n * BANK + (half + 1) * BANK // 2)
+                    nc.gpsimd.tensor_tensor(out=result[:, part], in0=result[:, part], in1=bd_all[:, part], op=ADD)
 
+        spread_bc()
+        append_partners(nc.gpsimd, bc_cols[:])
         for u in range(2):
             latent = wc_grouped[:, u * 256 : (u + 1) * 256, :].rearrange("q (p e) k -> q p k e", e=PAIR)
             rows = wc_raw[:].rearrange("q k (p u e) -> q u p k e", u=2, e=PAIR)[:, u]
@@ -299,11 +308,11 @@ def tile_deepseekmla_pa_t_kernel(tc, x, W_c, b_c, W_d, b_d, out):
         for k in range(SLOTS + 3):
             k_c, k_r, k_out = k - 1, k - 2, k - 3
             has_c, has_r, has_out = 0 <= k_c < SLOTS, 0 <= k_r < SLOTS, 0 <= k_out
+            if k < SLOTS + 2:
+                grouped[k] = work.tile([P, 2, SPAN * PACK], BF16, align_bytes=64, name="grouped")
             if k < SLOTS:
                 transpose_x(k)
             if k == 0:
-                spread_bias(0)
-                append_partners(nc.gpsimd, bc_cols[:])
                 fill_table()
                 rotate_bias(0)
             if has_r:
@@ -311,38 +320,29 @@ def tile_deepseekmla_pa_t_kernel(tc, x, W_c, b_c, W_d, b_d, out):
             if has_c:
                 paired_columns(k_c)
                 rotate(k_c)
-            vector_work = []
-            if k < SLOTS:
-                vector_work.append(lambda: quantise(x_codes, x_scales, grouped_x, k, "x"))
-            if has_r:
-                vector_work.append(lambda: quantise(r_codes, r_scales, grouped_r, k_r, "r"))
-            tail = k_out >= SLOTS - 2
             banks = []
             if has_out:
                 for a in range(SLOT_TILES):
                     result = results.tile([P, OUT], F32, name="result")
                     for n in (1, 0, 2):
-                        on_vector = n == 0 or (n == 2 and (tail or (k_out * SLOT_TILES + a) % 4 != 3))
-                        banks.append((a, n, on_vector, result))
+                        banks.append((a, n, result))
             for i in range(max(len(banks), SLOT_TILES)):
                 if has_c and i < SLOT_TILES:
                     other_columns(k_c, i)
                 if i < len(banks):
-                    a, n, on_vector, result = banks[i]
-                    second_product(k_out, a, n, on_vector, result)
+                    a, n, result = banks[i]
+                    second_product(k_out, a, n, n != 1, result)
                     if n == 2:
                         tile_of_group = k_out % 2 * SLOT_TILES + a
                         nc.sync.dma_start(out=out_groups[k_out // 2][:, tile_of_group, :], in_=result[:])
-                if i >= 1 and vector_work:
-                    vector_work.pop(0)()
-            for job in vector_work:
-                job()
+                if i == 1 and k < SLOTS + 2:
+                    quantise(k)
             if k == 1:
                 rotate_bias(1)
                 for n in (1, 0, 2):
                     regroup_wd(n)
             if k == 2:
                 for n in range(OUT_BANKS):
-                    spread_bias(1 + n)
+                    spread_bd(n)
                 for n in (1, 0, 2):
                     quantise_wd(n)

@@ -49,7 +49,7 @@ def tile_deepseekmla_pa_t_kernel(tc, x, W_c, b_c, W_d, b_d, out):
         consts = ctx.enter_context(tc.tile_pool(name="consts", bufs=1))
         work = ctx.enter_context(tc.tile_pool(name="work", bufs=3))
         results = ctx.enter_context(tc.tile_pool(name="results", bufs=10))
-        turn_psum = ctx.enter_context(tc.psum_pool(name="turn_psum", bufs=1))
+        turn_psum = ctx.enter_context(tc.psum_pool(name="turn_psum", bufs=2))
         c_psum = ctx.enter_context(tc.psum_pool(name="c_psum", bufs=2))
         out_psum = ctx.enter_context(tc.psum_pool(name="out_psum", bufs=4))
         ctx.enter_context(tc.manual_schedule())
@@ -171,16 +171,22 @@ def tile_deepseekmla_pa_t_kernel(tc, x, W_c, b_c, W_d, b_d, out):
         SPAN = SLOT_TILES * P
         grouped, codes, scales, r_rows, products = {}, {}, {}, {}, {}
 
-        def transpose_x(k):
-            words = x_sb[k // 2][:].bitcast(F32)
-            xt = turn_psum.tile([P, SLOT_TILES, 2, P], F32, tag="xt")
-            for a in range(SLOT_TILES):
+        def transpose(k, a):
+            turned = turn_psum.tile([P, 2, 2, P], F32, tag="turned")
+            if k < SLOTS:
+                words = x_sb[k // 2][:].bitcast(F32)
                 for u in range(2):
                     first = (k % 2 * SLOT_TILES + a) * 2 * P + u
-                    nc.tensor.transpose(xt[:, a, u, :], words[:, first : first + 2 * P - 1 : 2], ident[:])
+                    nc.tensor.transpose(turned[:, 0, u, :], words[:, first : first + 2 * P - 1 : 2], ident[:])
+            if k >= 2:
+                words = r_rows[k - 2][:].rearrange("n a u c -> n (a u c)").bitcast(F32)
+                for u in range(2):
+                    first = (a * 2 + u) * P
+                    nc.tensor.transpose(turned[:, 1, u, :], words[:, first : first + P], ident[:])
+            parts = slice(0 if k < SLOTS else 1, 2 if k >= 2 else 1)
             nc.scalar.copy(
-                out=grouped[k][:, 0].bitcast(F32).rearrange("q (a n u) -> q a n u", a=SLOT_TILES, u=2),
-                in_=xt[:].rearrange("q a u n -> q a n u"),
+                out=grouped[k][:].bitcast(F32).rearrange("p s (a n u) -> p s a n u", a=SLOT_TILES, u=2)[:, parts, a],
+                in_=turned[:, parts].rearrange("p s u n -> p s n u"),
             )
 
         def quantise(k):
@@ -241,18 +247,6 @@ def tile_deepseekmla_pa_t_kernel(tc, x, W_c, b_c, W_d, b_d, out):
                 op=ADD,
             )
 
-        def transpose_r(k):
-            words = r_rows[k][:].rearrange("n a u c -> n (a u c)").bitcast(F32)
-            rt = turn_psum.tile([P, SLOT_TILES, 2, P], F32, tag="rt")
-            for a in range(SLOT_TILES):
-                for u in range(2):
-                    first = (a * 2 + u) * P
-                    nc.tensor.transpose(rt[:, a, u, :], words[:, first : first + P], ident[:])
-            nc.scalar.copy(
-                out=grouped[k + 2][:, 1].bitcast(F32).rearrange("p (a n u) -> p a n u", a=SLOT_TILES, u=2),
-                in_=rt[:].rearrange("p a u n -> p a n u"),
-            )
-
         def second_product(k, a, n, on_vector, result):
             tokens = slice(a * P, (a + 1) * P)
             cols = slice(n * BANK, (n + 1) * BANK)
@@ -306,42 +300,42 @@ def tile_deepseekmla_pa_t_kernel(tc, x, W_c, b_c, W_d, b_d, out):
             nc.gpsimd.tensor_tensor(out=rotated_bias[:, at], in0=rotated_bias[:, at], in1=bias_part[:, at], op=ADD)
 
         for k in range(SLOTS + 3):
-            k_c, k_r, k_out = k - 1, k - 2, k - 3
-            has_c, has_r, has_out = 0 <= k_c < SLOTS, 0 <= k_r < SLOTS, 0 <= k_out
+            k_c, k_out = k - 1, k - 3
+            has_c, has_out = 0 <= k_c < SLOTS, 0 <= k_out
             if k < SLOTS + 2:
                 grouped[k] = work.tile([P, 2, SPAN * PACK], BF16, align_bytes=64, name="grouped")
-            if k < SLOTS:
-                transpose_x(k)
-            if k == 0:
-                fill_table()
-                rotate_bias(0)
-            if has_r:
-                transpose_r(k_r)
-            if has_c:
-                paired_columns(k_c)
-                rotate(k_c)
-            banks = []
-            if has_out:
-                for a in range(SLOT_TILES):
+            for a in range(SLOT_TILES):
+                if k < SLOTS + 2:
+                    transpose(k, a)
+                if k == 0 and a == 1:
+                    fill_table()
+                    rotate_bias(0)
+                if has_c:
+                    if a == 0:
+                        paired_columns(k_c)
+                        rotate(k_c)
+                    other_columns(k_c, a)
+                if has_out:
                     result = results.tile([P, OUT], F32, name="result")
-                    for n in (1, 0, 2):
-                        banks.append((a, n, result))
-            for i in range(max(len(banks), SLOT_TILES)):
-                if has_c and i < SLOT_TILES:
-                    other_columns(k_c, i)
-                if i < len(banks):
-                    a, n, result = banks[i]
-                    second_product(k_out, a, n, n != 1, result)
-                    if n == 2:
-                        tile_of_group = k_out % 2 * SLOT_TILES + a
-                        nc.sync.dma_start(out=out_groups[k_out // 2][:, tile_of_group, :], in_=result[:])
-                if i == 1 and k < SLOTS + 2:
+                    last_tile = k_out == SLOTS - 1 and a == SLOT_TILES - 1
+                    second_product(k_out, a, 1, last_tile, result)
+                if a == 1 and k < SLOTS + 2:
                     quantise(k)
+                if has_out:
+                    second_product(k_out, a, 0, True, result)
+                    second_product(k_out, a, 2, True, result)
+                    rows = out_groups[k_out // 2][:, k_out % 2 * SLOT_TILES + a, :]
+                    for n in (1, 0, 2) if last_tile else ():
+                        cols = slice(n * BANK, (n + 1) * BANK)
+                        nc.sync.dma_start(out=rows[:, cols], in_=result[:, cols])
+                    if not last_tile:
+                        nc.sync.dma_start(out=rows, in_=result[:])
             if k == 1:
                 rotate_bias(1)
-                for n in (1, 0, 2):
-                    regroup_wd(n)
+                regroup_wd(1)
+                regroup_wd(2)
             if k == 2:
+                regroup_wd(0)
                 for n in range(OUT_BANKS):
                     spread_bd(n)
                 for n in (1, 0, 2):

@@ -264,9 +264,7 @@ def tile_deepseekmla_pa_t_kernel(tc, x, W_c, b_c, W_d, b_d, out):
                 nc.vector.tensor_tensor(out=result[:, cols], in0=acc[:], in1=bd_all[:, cols], op=ADD)
             else:
                 nc.scalar.copy(out=result[:, cols], in_=acc[:])
-                for half in range(2):
-                    part = slice(n * BANK + half * BANK // 2, n * BANK + (half + 1) * BANK // 2)
-                    nc.gpsimd.tensor_tensor(out=result[:, part], in0=result[:, part], in1=bd_all[:, part], op=ADD)
+                nc.gpsimd.tensor_tensor(out=result[:, cols], in0=result[:, cols], in1=bd_all[:, cols], op=ADD)
 
         spread_bc()
         append_partners(nc.gpsimd, bc_cols[:])

@@ -13,6 +13,7 @@ FP8X4 = mybir.dt.float8_e4m3fn_x4
 ADD = mybir.AluOpType.add
 SUBTRACT = mybir.AluOpType.subtract
 MULT = mybir.AluOpType.mult
+IDENTITY = mybir.ActivationFunctionType.Identity
 SIN = mybir.ActivationFunctionType.Sin
 
 B, S, D, DC, DR, OUT = 4, 1024, 512, 512, 64, 1536
@@ -28,16 +29,24 @@ GROUPS = B * S // GROUP
 GROUPS_PER_SEQUENCE = S // GROUP
 SLOT_TILES = 2
 SLOTS = GROUPS * TILES // SLOT_TILES
+ORDERED = 4
 POSITIONS = GROUPS_PER_SEQUENCE * TILES
 BANK = 512
 OUT_BANKS = OUT // BANK
-ROT_P = DR // PACK
-FAR = ROT_P // 2
+TURNED = BANK
+LAST_BANK = OUT - BANK
+RESULT_BUFS = 7
+VECTOR_BANKS = 4
 ROT_U = DR // 2
-PAIRED = 2 * DR
 ROUND_MAGIC = 1.5 * 2.0**23
 
+R_STEPS = 3
+EARLY = (0, 1, SLOTS - 3, SLOTS - 2, SLOTS - 1)
 FLOPS = 2 * B * S * D * DC + 2 * B * S * DC * OUT
+
+
+def width_of_pass(columns):
+    return max(width for width in (64, 128, 256, BANK) if width <= columns)
 
 
 def tile_deepseekmla_pa_t_kernel(tc, x, W_c, b_c, W_d, b_d, out):
@@ -47,18 +56,18 @@ def tile_deepseekmla_pa_t_kernel(tc, x, W_c, b_c, W_d, b_d, out):
 
     with ExitStack() as ctx:
         consts = ctx.enter_context(tc.tile_pool(name="consts", bufs=1))
-        work = ctx.enter_context(tc.tile_pool(name="work", bufs=3))
-        results = ctx.enter_context(tc.tile_pool(name="results", bufs=10))
-        turn_psum = ctx.enter_context(tc.psum_pool(name="turn_psum", bufs=2))
-        c_psum = ctx.enter_context(tc.psum_pool(name="c_psum", bufs=2))
-        out_psum = ctx.enter_context(tc.psum_pool(name="out_psum", bufs=4))
+        work = ctx.enter_context(tc.tile_pool(name="work", bufs=4))
+        results = ctx.enter_context(tc.tile_pool(name="results", bufs=RESULT_BUFS))
+        vector_psum = ctx.enter_context(tc.psum_pool(name="vector_psum", bufs=VECTOR_BANKS))
+        scalar_psum = ctx.enter_context(tc.psum_pool(name="scalar_psum", bufs=8 - VECTOR_BANKS))
         ctx.enter_context(tc.manual_schedule())
 
         bc_rows = consts.tile([P, DC], BF16)
         nc.vector.memset(bc_rows[:].bitcast(I32), 0)
         nc.sync.dma_start(out=bc_rows[0:1, :], in_=b_c.unsqueeze(0))
         bd_rows = consts.tile([P, OUT], BF16)
-        nc.gpsimd.memset(bd_rows[:].bitcast(I32), 0)
+        nc.vector.memset(bd_rows[:].bitcast(I32), 0)
+        nc.sync.dma_start(out=bd_rows[0:1, :], in_=b_d.unsqueeze(0))
         wc_raw = consts.tile([P, PACK, DC], BF16)
         nc.sync.dma_start(out=wc_raw[:], in_=W_c.rearrange("(q k) c -> q k c", k=PACK))
         x_sb = []
@@ -66,13 +75,14 @@ def tile_deepseekmla_pa_t_kernel(tc, x, W_c, b_c, W_d, b_d, out):
             x_sb.append(consts.tile([P, TILES * D], BF16, name="x_sb%d" % g))
         nc.sync.dma_start(out=x_sb[0][:, 0 : 2 * D], in_=x_groups[0][:, 0 : 2 * D])
         nc.sync.dma_start(out=x_sb[0][:, 2 * D : 4 * D], in_=x_groups[0][:, 2 * D : 4 * D])
+        nc.sync.dma_start(out=x_sb[1][:, 0 : 2 * D], in_=x_groups[1][:, 0 : 2 * D])
         wd_raw = consts.tile([P, PACK, OUT], BF16)
         wd_rows = W_d.rearrange("(p t) c -> p t c", t=PACK)
         for n in range(OUT_BANKS):
             cols = slice(n * BANK, (n + 1) * BANK)
             nc.sync.dma_start(out=wd_raw[:, :, cols], in_=wd_rows[:, :, cols])
-        nc.sync.dma_start(out=bd_rows[0:1, :], in_=b_d.unsqueeze(0))
-        for g in range(1, GROUPS):
+        nc.sync.dma_start(out=x_sb[1][:, 2 * D : 4 * D], in_=x_groups[1][:, 2 * D : 4 * D])
+        for g in range(2, GROUPS):
             nc.sync.dma_start(out=x_sb[g][:], in_=x_groups[g])
 
         ones = consts.tile([P, P], BF16)
@@ -109,7 +119,7 @@ def tile_deepseekmla_pa_t_kernel(tc, x, W_c, b_c, W_d, b_d, out):
 
         def fill_table():
             turn = 2.0 * math.pi
-            for s, far, scale in ((0, 0, turn), (0, 1, turn), (1, 0, -turn), (1, 1, turn)):
+            for s, far, scale in ((0, 0, turn), (0, 1, turn), (1, 0, turn), (1, 1, -turn)):
                 nc.scalar.activation(
                     out=table[:, s].rearrange("p g (u h i) -> p (g u) h i", u=2, h=2)[:, :, far, :],
                     in_=turns[:, 1 - s].rearrange("p g (u i) -> p (g u) i", u=2),
@@ -117,14 +127,14 @@ def tile_deepseekmla_pa_t_kernel(tc, x, W_c, b_c, W_d, b_d, out):
                     scale=scale,
                 )
 
-        wc_grouped = consts.tile([P, DC + PAIRED, PACK], BF16, align_bytes=64)
-        wc_codes = consts.tile([P, DC + PAIRED], U32, align_bytes=64)
-        wc_scales = consts.tile([P, DC + PAIRED], U8, align_bytes=64)
-        bc_cols = consts.tile([P, DC + PAIRED, 1], F32)
+        wc_grouped = consts.tile([P, DC, PACK], BF16, align_bytes=64)
+        wc_codes = consts.tile([P, DC], U32, align_bytes=64)
+        wc_scales = consts.tile([P, DC], U8, align_bytes=64)
+        bc_cols = consts.tile([P, DC, 1], F32)
         bd_all = consts.tile([P, OUT], BF16)
 
         def spread_bc():
-            acc = out_psum.tile([P, BANK], F32, tag="out")
+            acc = scalar_psum.tile([P, BANK], F32, tag="bank")
             nc.tensor.matmul(acc[:], lhsT=ones[:], rhs=bc_rows[:], start=True, stop=True)
             for u in range(2):
                 nc.scalar.copy(
@@ -132,33 +142,33 @@ def tile_deepseekmla_pa_t_kernel(tc, x, W_c, b_c, W_d, b_d, out):
                     in_=acc[:].rearrange("n (p u e) -> n u p e", u=2, e=PAIR)[:, u],
                 )
 
+        bd_cols = consts.tile([P, 4], F32)
+
+        def spread_bd_cols():
+            acc = scalar_psum.tile([P, 4, 32], F32, tag="bank")
+            for half in range(4):
+                first = TURNED + half * P
+                nc.tensor.matmul(
+                    acc[:, half, :], lhsT=bd_rows[:, first : first + P], rhs=ones[:, 0:32], start=True, stop=True
+                )
+            nc.scalar.copy(out=bd_cols[:], in_=acc[:, :, 0])
+
         def spread_bd(n):
             cols = slice(n * BANK, (n + 1) * BANK)
-            acc = out_psum.tile([P, BANK], F32, tag="out")
+            acc = vector_psum.tile([P, BANK], F32, tag="bank")
             nc.tensor.matmul(acc[:], lhsT=ones[:], rhs=bd_rows[:, cols], start=True, stop=True)
-            nc.scalar.copy(out=bd_all[:, cols], in_=acc[:])
-
-        def append_partners(engine, cols):
-            halves = cols[:, 0:DC, :].rearrange("q (u c) w -> q u (c w)", u=2)
-            paired = cols[:, DC : DC + PAIRED, :].rearrange("q (s u c) w -> q s u (c w)", s=2, u=2)
-            mid = halves.shape[2] // 256 * PAIR * FAR
-            end = 2 * mid
-            engine.tensor_copy(out=paired[:, 0], in_=halves[:, :, 0:end])
-            engine.tensor_copy(out=paired[:, 1, :, 0:mid], in_=halves[:, :, mid:end])
-            engine.tensor_copy(out=paired[:, 1, :, mid:end], in_=halves[:, :, 0:mid])
+            return lambda: nc.scalar.copy(out=bd_all[:, cols], in_=acc[:])
 
         wd_grouped = consts.tile([P, OUT, PACK], BF16, align_bytes=64)
         wd_codes = consts.tile([P, OUT], U32, align_bytes=64)
         wd_scales = consts.tile([P, OUT], U8, align_bytes=64)
 
-        def regroup_wd(n):
-            cols = slice(n * BANK, (n + 1) * BANK)
-            wide = wd_grouped[:, cols, :].rearrange("p (c i) t -> p c t i", i=4)
-            rows = wd_raw[:, :, cols].rearrange("p t (c i) -> p c t i", i=4)
-            if n == 2:
-                nc.scalar.copy(out=wide, in_=rows)
-            else:
-                nc.vector.tensor_copy(out=wide, in_=rows)
+        def regroup_wd(copy, first, width):
+            cols = slice(first, first + width)
+            copy(
+                out=wd_grouped[:, cols, :].rearrange("p (c i) t -> p c t i", i=4),
+                in_=wd_raw[:, :, cols].rearrange("p t (c i) -> p c t i", i=4),
+            )
 
         def quantise_wd(n):
             cols = slice(n * BANK, (n + 1) * BANK)
@@ -169,28 +179,37 @@ def tile_deepseekmla_pa_t_kernel(tc, x, W_c, b_c, W_d, b_d, out):
             )
 
         SPAN = SLOT_TILES * P
+        result, sums = {}, {}
         grouped, codes, scales, r_rows, products = {}, {}, {}, {}, {}
 
-        def transpose(k, a):
-            turned = turn_psum.tile([P, 2, 2, P], F32, tag="turned")
-            if k < SLOTS:
-                words = x_sb[k // 2][:].bitcast(F32)
+        def turn_words(k, part, words):
+            turned = scalar_psum.tile([P, SLOT_TILES, 2, P], F32, tag="bank")
+            for a in range(SLOT_TILES):
                 for u in range(2):
-                    first = (k % 2 * SLOT_TILES + a) * 2 * P + u
-                    nc.tensor.transpose(turned[:, 0, u, :], words[:, first : first + 2 * P - 1 : 2], ident[:])
-            if k >= 2:
-                words = r_rows[k - 2][:].rearrange("n a u c -> n (a u c)").bitcast(F32)
-                for u in range(2):
-                    first = (a * 2 + u) * P
-                    nc.tensor.transpose(turned[:, 1, u, :], words[:, first : first + P], ident[:])
-            parts = slice(0 if k < SLOTS else 1, 2 if k >= 2 else 1)
+                    nc.tensor.transpose(turned[:, a, u, :], words[a][u], ident[:])
             nc.scalar.copy(
-                out=grouped[k][:].bitcast(F32).rearrange("p s (a n u) -> p s a n u", a=SLOT_TILES, u=2)[:, parts, a],
-                in_=turned[:, parts].rearrange("p s u n -> p s n u"),
+                out=grouped[k][:, part].bitcast(F32).rearrange("p (a n u) -> p a n u", a=SLOT_TILES, u=2),
+                in_=turned[:].rearrange("p a u n -> p a n u"),
+            )
+
+        def transpose_x(k):
+            words = x_sb[k // 2][:, k % 2 * SLOT_TILES * D : (k % 2 + 1) * SLOT_TILES * D].bitcast(F32)
+            turn_words(
+                k,
+                0,
+                [[words[:, 2 * P * a + u : 2 * P * a + u + 2 * P - 1 : 2] for u in range(2)] for a in range(SLOT_TILES)],
+            )
+
+        def transpose_r(k):
+            words = r_rows[k][:].rearrange("n a u c -> n (a u c)").bitcast(F32)
+            turn_words(
+                k + R_STEPS,
+                1,
+                [[words[:, P * (2 * a + u) : P * (2 * a + u + 1)] for u in range(2)] for a in range(SLOT_TILES)],
             )
 
         def quantise(k):
-            parts = slice(0 if k < SLOTS else 1, 2 if k >= 2 else 1)
+            parts = slice(0 if k < SLOTS else 1, 2 if k >= R_STEPS else 1)
             codes[k] = work.tile([P, 2, SPAN], U32, align_bytes=64, name="codes")
             scales[k] = work.tile([P, 2, SPAN], U8, align_bytes=64, name="scales")
             nc.vector.quantize_mx(
@@ -199,142 +218,225 @@ def tile_deepseekmla_pa_t_kernel(tc, x, W_c, b_c, W_d, b_d, out):
                 in_=grouped[k][:, parts].rearrange("p s n -> p (s n)"),
             )
 
-        def first_product(acc, k, a, cols):
+        def first_product(k, a):
+            at = (k * SLOT_TILES + a) % POSITIONS
+            if a == 0:
+                r_rows[k] = work.tile([P, SLOT_TILES, 2, 256], BF16, name="r_rows")
+                products[k] = work.tile([P, 2, SLOT_TILES, 2, ROT_U], F32, name="products")
             tokens = slice(a * P, (a + 1) * P)
+            c_acc = vector_psum.tile([P, 2, 256], F32, tag="bank")
             nc.tensor.matmul_mx(
-                out=acc,
+                out=c_acc[:].rearrange("n u c -> n (u c)"),
                 lhsT=codes[k][:, 0, tokens].bitcast(FP8X4),
                 lhsT_scale=scales[k][:, 0, tokens],
-                rhs=wc_codes[:, cols].bitcast(FP8X4),
-                rhs_scale=wc_scales[:, cols],
+                rhs=wc_codes[:].bitcast(FP8X4),
+                rhs_scale=wc_scales[:],
                 start=True,
                 stop=True,
             )
-
-        def paired_columns(k):
-            at = k * SLOT_TILES % POSITIONS
-            r_rows[k] = work.tile([P, SLOT_TILES, 2, 256], BF16, name="r_rows")
-            paired = c_psum.tile([P, SLOT_TILES, 2, DR], F32, tag="c")
-            for a in range(SLOT_TILES):
-                first_product(paired[:, a].rearrange("n s c -> n (s c)"), k, a, slice(DC, DC + PAIRED))
-            products[k] = work.tile([P, SLOT_TILES, 2, DR], F32, name="products")
             nc.vector.tensor_tensor(
-                out=products[k][:],
-                in0=paired[:],
-                in1=table[:, :, at : at + SLOT_TILES, :].rearrange("n s a c -> n a s c"),
+                out=products[k][:, :, a],
+                in0=c_acc[:, :, 0:ROT_U].unsqueeze(1).to_broadcast([P, 2, 2, ROT_U]),
+                in1=table[:, :, at, :].rearrange("n s (u c) -> n s u c", u=2),
                 op=MULT,
             )
+            nc.vector.tensor_tensor(
+                out=r_rows[k][:, a, :, ROT_U:256],
+                in0=c_acc[:, :, ROT_U:256],
+                in1=bc_cols[:, :, 0].rearrange("n (u c) -> n u c", u=2)[:, :, ROT_U:256],
+                op=ADD,
+            )
+
+        def swapped(cols):
+            return cols.rearrange("n t (h i) -> n t h i", h=2)[:, :, ::-1, :]
 
         def rotate(k):
             at = k * SLOT_TILES % POSITIONS
+            own = products[k][:, 0].rearrange("n a u c -> n (a u) c")
             nc.gpsimd.tensor_tensor(
-                out=products[k][:, :, 0, :], in0=products[k][:, :, 0, :], in1=products[k][:, :, 1, :], op=ADD
+                out=own.rearrange("n t (h i) -> n t h i", h=2),
+                in0=own.rearrange("n t (h i) -> n t h i", h=2),
+                in1=swapped(products[k][:, 1].rearrange("n a u c -> n (a u) c")),
+                op=ADD,
             )
             nc.gpsimd.tensor_tensor(
                 out=r_rows[k][:, :, :, 0:ROT_U],
-                in0=products[k][:, :, 0, :].rearrange("n a (u c) -> n a u c", u=2),
+                in0=products[k][:, 0],
                 in1=rotated_bias[:, at : at + SLOT_TILES, :].rearrange("n a (u c) -> n a u c", u=2),
                 op=ADD,
             )
 
-        def other_columns(k, a):
-            c_acc = c_psum.tile([P, 2, 256], F32, tag="c")
-            first_product(c_acc[:].rearrange("n u c -> n (u c)"), k, a, slice(0, DC))
-            nc.vector.tensor_tensor(
-                out=r_rows[k][:, a, :, ROT_U:256],
-                in0=c_acc[:, :, ROT_U:256],
-                in1=bc_cols[:, 0:DC, 0].rearrange("n (u c) -> n u c", u=2)[:, :, ROT_U:256],
-                op=ADD,
-            )
-
-        def second_product(k, a, n, on_vector, result):
+        def token_product(acc, k, a, cols):
             tokens = slice(a * P, (a + 1) * P)
-            cols = slice(n * BANK, (n + 1) * BANK)
-            acc = out_psum.tile([P, BANK], F32, tag="out")
             nc.tensor.matmul_mx(
-                out=acc[:],
-                lhsT=codes[k + 2][:, 1, tokens].bitcast(FP8X4),
-                lhsT_scale=scales[k + 2][:, 1, tokens],
+                out=acc,
+                lhsT=codes[k + R_STEPS][:, 1, tokens].bitcast(FP8X4),
+                lhsT_scale=scales[k + R_STEPS][:, 1, tokens],
                 rhs=wd_codes[:, cols].bitcast(FP8X4),
                 rhs_scale=wd_scales[:, cols],
                 start=True,
                 stop=True,
             )
-            if on_vector:
-                nc.vector.tensor_tensor(out=result[:, cols], in0=acc[:], in1=bd_all[:, cols], op=ADD)
-            else:
-                nc.scalar.copy(out=result[:, cols], in_=acc[:])
-                nc.gpsimd.tensor_tensor(out=result[:, cols], in0=result[:, cols], in1=bd_all[:, cols], op=ADD)
+
+
+        def product_bank(psum, k, a, first, width):
+            acc = psum.tile([P, BANK], F32, tag="bank")
+            done = 0
+            while done < width:
+                part = width_of_pass(width - done)
+                token_product(acc[:, done : done + part], k, a, slice(first + done, first + done + part))
+                done += part
+            return acc[:, 0:width]
+
+        def vector_bank(k, a, first, width):
+            acc = product_bank(vector_psum, k, a, first, width)
+            cols = slice(first, first + width)
+
+            def finish():
+                nc.vector.tensor_tensor(out=result[k][:, a, cols], in0=acc, in1=bd_all[:, cols], op=ADD)
+
+            return finish
+
+        def both_tiles(psum, k, first, width):
+            acc = psum.tile([P, SLOT_TILES, BANK // 2], F32, tag="bank")
+            for a in range(SLOT_TILES):
+                token_product(acc[:, a, 0:width], k, a, slice(first, first + width))
+            return acc[:, :, 0:width]
+
+        def add_bd(engine, k, cols, in0):
+            bias = bd_all[:, cols].unsqueeze(1).to_broadcast([P, SLOT_TILES, cols.stop - cols.start])
+            engine.tensor_tensor(out=result[k][:, :, cols], in0=in0, in1=bias, op=ADD)
+
+        def turned_columns(k):
+            sums[k] = work.tile([P, 4, SPAN], F32, name="sums")
+            for pair in range(4 // 2):
+                acc = scalar_psum.tile([P, 2, SPAN], F32, tag="bank")
+                for half in range(2):
+                    first = TURNED + (2 * pair + half) * P
+                    channels = slice(first, first + P)
+                    nc.tensor.matmul_mx(
+                        out=acc[:, half],
+                        lhsT=wd_codes[:, channels].bitcast(FP8X4),
+                        lhsT_scale=wd_scales[:, channels],
+                        rhs=codes[k + R_STEPS][:, 1].bitcast(FP8X4),
+                        rhs_scale=scales[k + R_STEPS][:, 1],
+                        start=True,
+                        stop=True,
+                    )
+                for half in range(2):
+                    b = 2 * pair + half
+                    nc.scalar.activation(
+                        out=sums[k][:, b], in_=acc[:, half], func=IDENTITY, bias=bd_cols[:, b : b + 1]
+                    )
+
+        def turn_back(k):
+            for pair in range(4 // 2):
+                acc = scalar_psum.tile([P, SLOT_TILES, 2, P], F32, tag="bank")
+                for a in range(SLOT_TILES):
+                    for half in range(2):
+                        nc.tensor.transpose(
+                            acc[:, a, half, :], sums[k][:, 2 * pair + half, a * P : (a + 1) * P], ident[:]
+                        )
+                first = TURNED + 2 * pair * P
+                nc.scalar.copy(out=result[k][:, :, first : first + 2 * P], in_=acc[:].rearrange("p a h c -> p a (h c)"))
+
+        def store(k, a, cols):
+            nc.sync.dma_start(
+                out=out_groups[k // 2][:, k % 2 * SLOT_TILES + a, cols], in_=result[k][:, a, cols]
+            )
 
         spread_bc()
-        append_partners(nc.gpsimd, bc_cols[:])
+        spread_bd_cols()
+        bd_copies = [spread_bd(n) for n in range(OUT_BANKS)]
         for u in range(2):
             latent = wc_grouped[:, u * 256 : (u + 1) * 256, :].rearrange("q (p e) k -> q p k e", e=PAIR)
             rows = wc_raw[:].rearrange("q k (p u e) -> q u p k e", u=2, e=PAIR)[:, u]
-            if u == 0:
-                nc.vector.tensor_copy(out=latent, in_=rows)
-            else:
-                nc.scalar.copy(out=latent, in_=rows)
-        append_partners(nc.vector, wc_grouped[:])
-        for cols in (slice(DC, DC + PAIRED), slice(0, DC)):
-            nc.vector.quantize_mx(
-                out=wc_codes[:, cols].bitcast(FP8X4),
-                scales=wc_scales[:, cols],
-                in_=wc_grouped[:, cols, :].rearrange("q c k -> q (c k)"),
-            )
+            nc.vector.tensor_copy(out=latent, in_=rows)
+        nc.vector.quantize_mx(
+            out=wc_codes[:].bitcast(FP8X4), scales=wc_scales[:], in_=wc_grouped[:].rearrange("q c k -> q (c k)")
+        )
         rotated_bias = consts.tile([P, POSITIONS, DR], F32)
         bias_part = consts.tile([P, POSITIONS, DR], F32)
 
         def rotate_bias(h):
             at = slice(h * TILES, (h + 1) * TILES)
+            bias = bc_cols[:, :, 0].rearrange("n (u c) -> n u c", u=2)[:, :, 0:ROT_U]
             for s, into in ((0, rotated_bias), (1, bias_part)):
-                pair_bias = bc_cols[:, DC + s * DR : DC + (s + 1) * DR, 0]
                 nc.gpsimd.tensor_tensor(
-                    out=into[:, at],
-                    in0=table[:, s, at],
-                    in1=pair_bias.unsqueeze(1).to_broadcast([P, TILES, DR]),
+                    out=into[:, at].rearrange("n a (u c) -> n a u c", u=2),
+                    in0=table[:, s, at].rearrange("n a (u c) -> n a u c", u=2),
+                    in1=bias.unsqueeze(1).to_broadcast([P, TILES, 2, ROT_U]),
                     op=MULT,
                 )
-            nc.gpsimd.tensor_tensor(out=rotated_bias[:, at], in0=rotated_bias[:, at], in1=bias_part[:, at], op=ADD)
+            total = rotated_bias[:, at].rearrange("n a (u c) -> n (a u) c", u=2)
+            nc.gpsimd.tensor_tensor(
+                out=total.rearrange("n t (h i) -> n t h i", h=2),
+                in0=total.rearrange("n t (h i) -> n t h i", h=2),
+                in1=swapped(bias_part[:, at].rearrange("n a (u c) -> n (a u) c", u=2)),
+                op=ADD,
+            )
 
-        for k in range(SLOTS + 3):
-            k_c, k_out = k - 1, k - 3
-            has_c, has_out = 0 <= k_c < SLOTS, 0 <= k_out
-            if k < SLOTS + 2:
-                grouped[k] = work.tile([P, 2, SPAN * PACK], BF16, align_bytes=64, name="grouped")
-            for a in range(SLOT_TILES):
-                if k < SLOTS + 2:
-                    transpose(k, a)
-                if k == 0 and a == 1:
-                    fill_table()
-                    rotate_bias(0)
-                if has_c:
-                    if a == 0:
-                        paired_columns(k_c)
-                        rotate(k_c)
-                    other_columns(k_c, a)
-                if has_out:
-                    result = results.tile([P, OUT], F32, name="result")
-                    last_tile = k_out == SLOTS - 1 and a == SLOT_TILES - 1
-                    second_product(k_out, a, 1, last_tile, result)
-                if a == 1 and k < SLOTS + 2:
-                    quantise(k)
-                if has_out:
-                    second_product(k_out, a, 0, True, result)
-                    second_product(k_out, a, 2, True, result)
-                    rows = out_groups[k_out // 2][:, k_out % 2 * SLOT_TILES + a, :]
-                    for n in (1, 0, 2) if last_tile else ():
-                        cols = slice(n * BANK, (n + 1) * BANK)
-                        nc.sync.dma_start(out=rows[:, cols], in_=result[:, cols])
-                    if not last_tile:
-                        nc.sync.dma_start(out=rows, in_=result[:])
-            if k == 1:
-                rotate_bias(1)
-                regroup_wd(1)
-                regroup_wd(2)
+        waiting = []
+        for k in range(SLOTS + R_STEPS + 2):
+            k_c, k_r, k_out, k_done = k - 1, k - R_STEPS, k - R_STEPS - 1, k - R_STEPS - 2
+            has_c, has_r, has_out, has_done = 0 <= k_c < SLOTS, 0 <= k_r < SLOTS, 0 <= k_out < SLOTS, 0 <= k_done
+            plain = k_out == SLOTS - 1
+            if 1 <= k < SLOTS + R_STEPS + 1:
+                quantise(k - 1)
+            for finish, k_wait, a, cols in waiting:
+                finish()
+                if k_wait in EARLY:
+                    store(k_wait, a, cols)
+            waiting = []
             if k == 2:
-                regroup_wd(0)
-                for n in range(OUT_BANKS):
-                    spread_bd(n)
-                for n in (1, 0, 2):
-                    quantise_wd(n)
+                regroup_wd(nc.vector.tensor_copy, 0, BANK)
+            if k < SLOTS + R_STEPS:
+                grouped[k] = work.tile([P, 2, SPAN * PACK], BF16, align_bytes=64, name="grouped")
+            if k < SLOTS:
+                transpose_x(k)
+            if has_r:
+                transpose_r(k_r)
+            if has_done:
+                if k_done < SLOTS - 1:
+                    turn_back(k_done)
+            if k == 0:
+                fill_table()
+                rotate_bias(0)
+            if k == 3:
+                quantise_wd(0)
+                quantise_wd(1)
+            if has_done:
+                for a in range(SLOT_TILES):
+                    for cols in (slice(BANK, LAST_BANK),) if k_done in EARLY else (slice(0, OUT),):
+                        store(k_done, a, cols)
+            if has_c:
+                for a in range(SLOT_TILES):
+                    first_product(k_c, a)
+                rotate(k_c)
+            if has_out:
+                result[k_out] = results.tile([P, SLOT_TILES, OUT], F32, name="result")
+                if plain:
+                    for first in range(TURNED, LAST_BANK, 2 * P):
+                        acc = both_tiles(vector_psum, k_out, first, 2 * P)
+                        add_bd(nc.vector, k_out, slice(first, first + 2 * P), acc)
+                else:
+                    turned_columns(k_out)
+                for a in range(SLOT_TILES):
+                    for first, width in ((0, BANK), (LAST_BANK, OUT - LAST_BANK)):
+                        finish = vector_bank(k_out, a, first, width)
+                        if plain or a == 0:
+                            finish()
+                            if k_out in EARLY:
+                                store(k_out, a, slice(first, first + width))
+                        else:
+                            waiting.append((finish, k_out, a, slice(first, first + width)))
+            if k == 1:
+                for copy in bd_copies:
+                    copy()
+                regroup_wd(nc.scalar.copy, BANK, BANK)
+            if k == 2:
+                rotate_bias(1)
+                regroup_wd(nc.scalar.copy, 2 * BANK, BANK // 2)
+                regroup_wd(nc.vector.tensor_copy, 5 * BANK // 2, BANK // 2)
+            if k == 3:
+                quantise_wd(2)

@@ -29,24 +29,19 @@ GROUPS = B * S // GROUP
 GROUPS_PER_SEQUENCE = S // GROUP
 SLOT_TILES = 2
 SLOTS = GROUPS * TILES // SLOT_TILES
-ORDERED = 4
 POSITIONS = GROUPS_PER_SEQUENCE * TILES
 BANK = 512
 OUT_BANKS = OUT // BANK
-TURNED = BANK
-LAST_BANK = OUT - BANK
-RESULT_BUFS = 7
+VECTOR_COLS = 2 * BANK
+TURNED_BLOCKS = (OUT - VECTOR_COLS) // P
+RESULT_BUFS = 6
 VECTOR_BANKS = 4
 ROT_U = DR // 2
 ROUND_MAGIC = 1.5 * 2.0**23
+C_LAG, R_LAG, OUT_LAG, BACK_LAG = 1, 3, 4, 5
+ORDERED = 6
 
-R_STEPS = 3
-EARLY = (0, 1, SLOTS - 3, SLOTS - 2, SLOTS - 1)
 FLOPS = 2 * B * S * D * DC + 2 * B * S * DC * OUT
-
-
-def width_of_pass(columns):
-    return max(width for width in (64, 128, 256, BANK) if width <= columns)
 
 
 def tile_deepseekmla_pa_t_kernel(tc, x, W_c, b_c, W_d, b_d, out):
@@ -73,17 +68,21 @@ def tile_deepseekmla_pa_t_kernel(tc, x, W_c, b_c, W_d, b_d, out):
         x_sb = []
         for g in range(GROUPS):
             x_sb.append(consts.tile([P, TILES * D], BF16, name="x_sb%d" % g))
-        nc.sync.dma_start(out=x_sb[0][:, 0 : 2 * D], in_=x_groups[0][:, 0 : 2 * D])
-        nc.sync.dma_start(out=x_sb[0][:, 2 * D : 4 * D], in_=x_groups[0][:, 2 * D : 4 * D])
-        nc.sync.dma_start(out=x_sb[1][:, 0 : 2 * D], in_=x_groups[1][:, 0 : 2 * D])
+
+        def load_x(g, first, tiles):
+            cols = slice(first * D, (first + tiles) * D)
+            nc.sync.dma_start(out=x_sb[g][:, cols], in_=x_groups[g][:, cols])
+
+        for k in range(3):
+            load_x(k // 2, k % 2 * SLOT_TILES, SLOT_TILES)
         wd_raw = consts.tile([P, PACK, OUT], BF16)
         wd_rows = W_d.rearrange("(p t) c -> p t c", t=PACK)
         for n in range(OUT_BANKS):
             cols = slice(n * BANK, (n + 1) * BANK)
             nc.sync.dma_start(out=wd_raw[:, :, cols], in_=wd_rows[:, :, cols])
-        nc.sync.dma_start(out=x_sb[1][:, 2 * D : 4 * D], in_=x_groups[1][:, 2 * D : 4 * D])
+        load_x(1, SLOT_TILES, SLOT_TILES)
         for g in range(2, GROUPS):
-            nc.sync.dma_start(out=x_sb[g][:], in_=x_groups[g])
+            load_x(g, 0, TILES)
 
         ones = consts.tile([P, P], BF16)
         nc.vector.memset(ones[:], 1.0)
@@ -127,29 +126,25 @@ def tile_deepseekmla_pa_t_kernel(tc, x, W_c, b_c, W_d, b_d, out):
                     scale=scale,
                 )
 
-        wc_grouped = consts.tile([P, DC, PACK], BF16, align_bytes=64)
-        wc_codes = consts.tile([P, DC], U32, align_bytes=64)
-        wc_scales = consts.tile([P, DC], U8, align_bytes=64)
-        bc_cols = consts.tile([P, DC, 1], F32)
+        bc_cols = consts.tile([P, 2, 256], F32)
         bd_all = consts.tile([P, OUT], BF16)
+        bd_cols = consts.tile([P, TURNED_BLOCKS], F32)
 
         def spread_bc():
             acc = scalar_psum.tile([P, BANK], F32, tag="bank")
             nc.tensor.matmul(acc[:], lhsT=ones[:], rhs=bc_rows[:], start=True, stop=True)
             for u in range(2):
                 nc.scalar.copy(
-                    out=bc_cols[:, u * 256 : (u + 1) * 256, 0].rearrange("n (p e) -> n p e", e=PAIR),
+                    out=bc_cols[:, u].rearrange("n (p e) -> n p e", e=PAIR),
                     in_=acc[:].rearrange("n (p u e) -> n u p e", u=2, e=PAIR)[:, u],
                 )
 
-        bd_cols = consts.tile([P, 4], F32)
-
         def spread_bd_cols():
-            acc = scalar_psum.tile([P, 4, 32], F32, tag="bank")
-            for half in range(4):
-                first = TURNED + half * P
+            acc = scalar_psum.tile([P, TURNED_BLOCKS, 32], F32, tag="bank")
+            for block in range(TURNED_BLOCKS):
+                first = VECTOR_COLS + block * P
                 nc.tensor.matmul(
-                    acc[:, half, :], lhsT=bd_rows[:, first : first + P], rhs=ones[:, 0:32], start=True, stop=True
+                    acc[:, block, :], lhsT=bd_rows[:, first : first + P], rhs=ones[:, 0:32], start=True, stop=True
                 )
             nc.scalar.copy(out=bd_cols[:], in_=acc[:, :, 0])
 
@@ -158,6 +153,42 @@ def tile_deepseekmla_pa_t_kernel(tc, x, W_c, b_c, W_d, b_d, out):
             acc = vector_psum.tile([P, BANK], F32, tag="bank")
             nc.tensor.matmul(acc[:], lhsT=ones[:], rhs=bd_rows[:, cols], start=True, stop=True)
             return lambda: nc.scalar.copy(out=bd_all[:, cols], in_=acc[:])
+
+        rotated_bias = consts.tile([P, POSITIONS, DR], F32)
+        bias_part = consts.tile([P, POSITIONS, DR], F32)
+
+        def swapped(cols):
+            return cols.rearrange("n t (h i) -> n t h i", h=2)[:, :, ::-1, :]
+
+        def rotate_bias():
+            for s, into in ((0, rotated_bias), (1, bias_part)):
+                nc.vector.tensor_tensor(
+                    out=into[:].rearrange("n a (u c) -> n a u c", u=2),
+                    in0=table[:, s].rearrange("n a (u c) -> n a u c", u=2),
+                    in1=bc_cols[:, :, 0:ROT_U].unsqueeze(1).to_broadcast([P, POSITIONS, 2, ROT_U]),
+                    op=MULT,
+                )
+            total = rotated_bias[:].rearrange("n a (u c) -> n (a u) c", u=2)
+            nc.vector.tensor_tensor(
+                out=total.rearrange("n t (h i) -> n t h i", h=2),
+                in0=total.rearrange("n t (h i) -> n t h i", h=2),
+                in1=swapped(bias_part[:].rearrange("n a (u c) -> n (a u) c", u=2)),
+                op=ADD,
+            )
+
+        wc_grouped = consts.tile([P, DC, PACK], BF16, align_bytes=64)
+        wc_codes = consts.tile([P, DC], U32, align_bytes=64)
+        wc_scales = consts.tile([P, DC], U8, align_bytes=64)
+
+        def prepare_wc():
+            for u in range(2):
+                nc.vector.tensor_copy(
+                    out=wc_grouped[:, u * 256 : (u + 1) * 256, :].rearrange("q (p e) k -> q p k e", e=PAIR),
+                    in_=wc_raw[:].rearrange("q k (p u e) -> q u p k e", u=2, e=PAIR)[:, u],
+                )
+            nc.vector.quantize_mx(
+                out=wc_codes[:].bitcast(FP8X4), scales=wc_scales[:], in_=wc_grouped[:].rearrange("q c k -> q (c k)")
+            )
 
         wd_grouped = consts.tile([P, OUT, PACK], BF16, align_bytes=64)
         wd_codes = consts.tile([P, OUT], U32, align_bytes=64)
@@ -179,8 +210,7 @@ def tile_deepseekmla_pa_t_kernel(tc, x, W_c, b_c, W_d, b_d, out):
             )
 
         SPAN = SLOT_TILES * P
-        result, sums = {}, {}
-        grouped, codes, scales, r_rows, products = {}, {}, {}, {}, {}
+        x_words, grouped, codes, scales, products, r_rows, sums, result = {}, {}, {}, {}, {}, {}, {}, {}
 
         def turn_words(k, part, words):
             turned = scalar_psum.tile([P, SLOT_TILES, 2, P], F32, tag="bank")
@@ -192,24 +222,28 @@ def tile_deepseekmla_pa_t_kernel(tc, x, W_c, b_c, W_d, b_d, out):
                 in_=turned[:].rearrange("p a u n -> p a n u"),
             )
 
+        def words_of_x(k):
+            first = k % 2 * SLOT_TILES * D
+            return x_sb[k // 2][:, first : first + SLOT_TILES * D].bitcast(F32)
+
+        def order_words(k):
+            x_words[k] = work.tile([P, SLOT_TILES, 2, P], F32, name="x_words")
+            nc.scalar.copy(out=x_words[k][:], in_=words_of_x(k).rearrange("n (a q u) -> n a u q", a=SLOT_TILES, u=2))
+
         def transpose_x(k):
-            words = x_sb[k // 2][:, k % 2 * SLOT_TILES * D : (k % 2 + 1) * SLOT_TILES * D].bitcast(F32)
-            turn_words(
-                k,
-                0,
-                [[words[:, 2 * P * a + u : 2 * P * a + u + 2 * P - 1 : 2] for u in range(2)] for a in range(SLOT_TILES)],
-            )
+            if k < ORDERED:
+                words = words_of_x(k).rearrange("n (a q u) -> n a u q", a=SLOT_TILES, u=2)
+            else:
+                words = x_words[k]
+            turn_words(k, 0, [[words[:, a, u, :] for u in range(2)] for a in range(SLOT_TILES)])
 
         def transpose_r(k):
             words = r_rows[k][:].rearrange("n a u c -> n (a u c)").bitcast(F32)
-            turn_words(
-                k + R_STEPS,
-                1,
-                [[words[:, P * (2 * a + u) : P * (2 * a + u + 1)] for u in range(2)] for a in range(SLOT_TILES)],
-            )
+            words = words.rearrange("n (a u q) -> n a u q", a=SLOT_TILES, u=2)
+            turn_words(k + R_LAG, 1, [[words[:, a, u, :] for u in range(2)] for a in range(SLOT_TILES)])
 
         def quantise(k):
-            parts = slice(0 if k < SLOTS else 1, 2 if k >= R_STEPS else 1)
+            parts = slice(0 if k < SLOTS else 1, 2 if k >= R_LAG else 1)
             codes[k] = work.tile([P, 2, SPAN], U32, align_bytes=64, name="codes")
             scales[k] = work.tile([P, 2, SPAN], U8, align_bytes=64, name="scales")
             nc.vector.quantize_mx(
@@ -220,9 +254,6 @@ def tile_deepseekmla_pa_t_kernel(tc, x, W_c, b_c, W_d, b_d, out):
 
         def first_product(k, a):
             at = (k * SLOT_TILES + a) % POSITIONS
-            if a == 0:
-                r_rows[k] = work.tile([P, SLOT_TILES, 2, 256], BF16, name="r_rows")
-                products[k] = work.tile([P, 2, SLOT_TILES, 2, ROT_U], F32, name="products")
             tokens = slice(a * P, (a + 1) * P)
             c_acc = vector_psum.tile([P, 2, 256], F32, tag="bank")
             nc.tensor.matmul_mx(
@@ -241,14 +272,8 @@ def tile_deepseekmla_pa_t_kernel(tc, x, W_c, b_c, W_d, b_d, out):
                 op=MULT,
             )
             nc.vector.tensor_tensor(
-                out=r_rows[k][:, a, :, ROT_U:256],
-                in0=c_acc[:, :, ROT_U:256],
-                in1=bc_cols[:, :, 0].rearrange("n (u c) -> n u c", u=2)[:, :, ROT_U:256],
-                op=ADD,
+                out=r_rows[k][:, a, :, ROT_U:256], in0=c_acc[:, :, ROT_U:256], in1=bc_cols[:, :, ROT_U:256], op=ADD
             )
-
-        def swapped(cols):
-            return cols.rearrange("n t (h i) -> n t h i", h=2)[:, :, ::-1, :]
 
         def rotate(k):
             at = k * SLOT_TILES % POSITIONS
@@ -266,177 +291,136 @@ def tile_deepseekmla_pa_t_kernel(tc, x, W_c, b_c, W_d, b_d, out):
                 op=ADD,
             )
 
+
         def token_product(acc, k, a, cols):
             tokens = slice(a * P, (a + 1) * P)
             nc.tensor.matmul_mx(
                 out=acc,
-                lhsT=codes[k + R_STEPS][:, 1, tokens].bitcast(FP8X4),
-                lhsT_scale=scales[k + R_STEPS][:, 1, tokens],
+                lhsT=codes[k + R_LAG][:, 1, tokens].bitcast(FP8X4),
+                lhsT_scale=scales[k + R_LAG][:, 1, tokens],
                 rhs=wd_codes[:, cols].bitcast(FP8X4),
                 rhs_scale=wd_scales[:, cols],
                 start=True,
                 stop=True,
             )
 
-
-        def product_bank(psum, k, a, first, width):
-            acc = psum.tile([P, BANK], F32, tag="bank")
-            done = 0
-            while done < width:
-                part = width_of_pass(width - done)
-                token_product(acc[:, done : done + part], k, a, slice(first + done, first + done + part))
-                done += part
-            return acc[:, 0:width]
-
-        def vector_bank(k, a, first, width):
-            acc = product_bank(vector_psum, k, a, first, width)
-            cols = slice(first, first + width)
+        def vector_banks(k, a):
+            accs = []
+            for first in range(0, VECTOR_COLS, BANK):
+                acc = vector_psum.tile([P, BANK], F32, tag="bank")
+                token_product(acc[:], k, a, slice(first, first + BANK))
+                accs.append(acc)
 
             def finish():
-                nc.vector.tensor_tensor(out=result[k][:, a, cols], in0=acc, in1=bd_all[:, cols], op=ADD)
+                for i in range(len(accs)):
+                    cols = slice(i * BANK, (i + 1) * BANK)
+                    nc.vector.tensor_tensor(out=result[k][:, a, cols], in0=accs[i][:], in1=bd_all[:, cols], op=ADD)
+                nc.sync.dma_start(out=out_rows(k)[:, a, 0:VECTOR_COLS], in_=result[k][:, a, 0:VECTOR_COLS])
 
             return finish
 
-        def both_tiles(psum, k, first, width):
-            acc = psum.tile([P, SLOT_TILES, BANK // 2], F32, tag="bank")
-            for a in range(SLOT_TILES):
-                token_product(acc[:, a, 0:width], k, a, slice(first, first + width))
-            return acc[:, :, 0:width]
-
-        def add_bd(engine, k, cols, in0):
-            bias = bd_all[:, cols].unsqueeze(1).to_broadcast([P, SLOT_TILES, cols.stop - cols.start])
-            engine.tensor_tensor(out=result[k][:, :, cols], in0=in0, in1=bias, op=ADD)
-
         def turned_columns(k):
-            sums[k] = work.tile([P, 4, SPAN], F32, name="sums")
-            for pair in range(4 // 2):
+            sums[k] = work.tile([P, TURNED_BLOCKS, SPAN], F32, name="sums")
+            for pair in range(0, TURNED_BLOCKS, 2):
                 acc = scalar_psum.tile([P, 2, SPAN], F32, tag="bank")
-                for half in range(2):
-                    first = TURNED + (2 * pair + half) * P
+                for i in range(2):
+                    first = VECTOR_COLS + (pair + i) * P
                     channels = slice(first, first + P)
                     nc.tensor.matmul_mx(
-                        out=acc[:, half],
+                        out=acc[:, i],
                         lhsT=wd_codes[:, channels].bitcast(FP8X4),
                         lhsT_scale=wd_scales[:, channels],
-                        rhs=codes[k + R_STEPS][:, 1].bitcast(FP8X4),
-                        rhs_scale=scales[k + R_STEPS][:, 1],
+                        rhs=codes[k + R_LAG][:, 1].bitcast(FP8X4),
+                        rhs_scale=scales[k + R_LAG][:, 1],
                         start=True,
                         stop=True,
                     )
-                for half in range(2):
-                    b = 2 * pair + half
+                for i in range(2):
+                    block = pair + i
                     nc.scalar.activation(
-                        out=sums[k][:, b], in_=acc[:, half], func=IDENTITY, bias=bd_cols[:, b : b + 1]
+                        out=sums[k][:, block], in_=acc[:, i], func=IDENTITY, bias=bd_cols[:, block : block + 1]
                     )
 
         def turn_back(k):
-            for pair in range(4 // 2):
+            for pair in range(0, TURNED_BLOCKS, 2):
                 acc = scalar_psum.tile([P, SLOT_TILES, 2, P], F32, tag="bank")
                 for a in range(SLOT_TILES):
-                    for half in range(2):
-                        nc.tensor.transpose(
-                            acc[:, a, half, :], sums[k][:, 2 * pair + half, a * P : (a + 1) * P], ident[:]
-                        )
-                first = TURNED + 2 * pair * P
-                nc.scalar.copy(out=result[k][:, :, first : first + 2 * P], in_=acc[:].rearrange("p a h c -> p a (h c)"))
+                    for i in range(2):
+                        nc.tensor.transpose(acc[:, a, i, :], sums[k][:, pair + i, a * P : (a + 1) * P], ident[:])
+                first = VECTOR_COLS + pair * P
+                nc.scalar.copy(
+                    out=result[k][:, :, first : first + 2 * P], in_=acc[:].rearrange("p a i c -> p a (i c)")
+                )
 
-        def store(k, a, cols):
-            nc.sync.dma_start(
-                out=out_groups[k // 2][:, k % 2 * SLOT_TILES + a, cols], in_=result[k][:, a, cols]
-            )
+        def straight_columns(k):
+            for first in range(VECTOR_COLS, OUT, 2 * P):
+                cols = slice(first, first + 2 * P)
+                acc = vector_psum.tile([P, SLOT_TILES, 2 * P], F32, tag="bank")
+                for a in range(SLOT_TILES):
+                    token_product(acc[:, a], k, a, cols)
+                bias = bd_all[:, cols].unsqueeze(1).to_broadcast([P, SLOT_TILES, 2 * P])
+                nc.vector.tensor_tensor(out=result[k][:, :, cols], in0=acc[:], in1=bias, op=ADD)
+
+        def out_rows(k):
+            first = k % 2 * SLOT_TILES
+            return out_groups[k // 2][:, first : first + SLOT_TILES, :]
+
+        def store_turned(k):
+            nc.sync.dma_start(out=out_rows(k)[:, :, VECTOR_COLS:OUT], in_=result[k][:, :, VECTOR_COLS:OUT])
 
         spread_bc()
         spread_bd_cols()
         bd_copies = [spread_bd(n) for n in range(OUT_BANKS)]
-        for u in range(2):
-            latent = wc_grouped[:, u * 256 : (u + 1) * 256, :].rearrange("q (p e) k -> q p k e", e=PAIR)
-            rows = wc_raw[:].rearrange("q k (p u e) -> q u p k e", u=2, e=PAIR)[:, u]
-            nc.vector.tensor_copy(out=latent, in_=rows)
-        nc.vector.quantize_mx(
-            out=wc_codes[:].bitcast(FP8X4), scales=wc_scales[:], in_=wc_grouped[:].rearrange("q c k -> q (c k)")
-        )
-        rotated_bias = consts.tile([P, POSITIONS, DR], F32)
-        bias_part = consts.tile([P, POSITIONS, DR], F32)
-
-        def rotate_bias(h):
-            at = slice(h * TILES, (h + 1) * TILES)
-            bias = bc_cols[:, :, 0].rearrange("n (u c) -> n u c", u=2)[:, :, 0:ROT_U]
-            for s, into in ((0, rotated_bias), (1, bias_part)):
-                nc.gpsimd.tensor_tensor(
-                    out=into[:, at].rearrange("n a (u c) -> n a u c", u=2),
-                    in0=table[:, s, at].rearrange("n a (u c) -> n a u c", u=2),
-                    in1=bias.unsqueeze(1).to_broadcast([P, TILES, 2, ROT_U]),
-                    op=MULT,
-                )
-            total = rotated_bias[:, at].rearrange("n a (u c) -> n (a u) c", u=2)
-            nc.gpsimd.tensor_tensor(
-                out=total.rearrange("n t (h i) -> n t h i", h=2),
-                in0=total.rearrange("n t (h i) -> n t h i", h=2),
-                in1=swapped(bias_part[:, at].rearrange("n a (u c) -> n (a u) c", u=2)),
-                op=ADD,
-            )
-
+        fill_table()
+        prepare_wc()
         waiting = []
-        for k in range(SLOTS + R_STEPS + 2):
-            k_c, k_r, k_out, k_done = k - 1, k - R_STEPS, k - R_STEPS - 1, k - R_STEPS - 2
-            has_c, has_r, has_out, has_done = 0 <= k_c < SLOTS, 0 <= k_r < SLOTS, 0 <= k_out < SLOTS, 0 <= k_done
-            plain = k_out == SLOTS - 1
-            if 1 <= k < SLOTS + R_STEPS + 1:
+        for k in range(SLOTS + BACK_LAG):
+            k_c, k_r, k_out, k_back = k - C_LAG, k - R_LAG, k - OUT_LAG, k - BACK_LAG
+            if 1 <= k <= SLOTS - 1 + OUT_LAG:
                 quantise(k - 1)
-            for finish, k_wait, a, cols in waiting:
+            if k == OUT_LAG:
+                quantise_wd(2)
+            if k == C_LAG:
+                rotate_bias()
+            for finish in waiting:
                 finish()
-                if k_wait in EARLY:
-                    store(k_wait, a, cols)
             waiting = []
             if k == 2:
                 regroup_wd(nc.vector.tensor_copy, 0, BANK)
-            if k < SLOTS + R_STEPS:
+            if k < SLOTS + R_LAG:
                 grouped[k] = work.tile([P, 2, SPAN * PACK], BF16, align_bytes=64, name="grouped")
             if k < SLOTS:
                 transpose_x(k)
-            if has_r:
+            if 0 <= k_r < SLOTS:
                 transpose_r(k_r)
-            if has_done:
-                if k_done < SLOTS - 1:
-                    turn_back(k_done)
-            if k == 0:
-                fill_table()
-                rotate_bias(0)
-            if k == 3:
+            if 0 <= k_back < SLOTS - 1:
+                turn_back(k_back)
+                store_turned(k_back)
+            if k == R_LAG:
                 quantise_wd(0)
                 quantise_wd(1)
-            if has_done:
-                for a in range(SLOT_TILES):
-                    for cols in (slice(BANK, LAST_BANK),) if k_done in EARLY else (slice(0, OUT),):
-                        store(k_done, a, cols)
-            if has_c:
+            if ORDERED <= k + 2 < SLOTS:
+                order_words(k + 2)
+            if 0 <= k_c < SLOTS:
+                r_rows[k_c] = work.tile([P, SLOT_TILES, 2, 256], BF16, name="r_rows")
+                products[k_c] = work.tile([P, 2, SLOT_TILES, 2, ROT_U], F32, name="products")
                 for a in range(SLOT_TILES):
                     first_product(k_c, a)
                 rotate(k_c)
-            if has_out:
+            if 0 <= k_out < SLOTS:
                 result[k_out] = results.tile([P, SLOT_TILES, OUT], F32, name="result")
-                if plain:
-                    for first in range(TURNED, LAST_BANK, 2 * P):
-                        acc = both_tiles(vector_psum, k_out, first, 2 * P)
-                        add_bd(nc.vector, k_out, slice(first, first + 2 * P), acc)
-                else:
+                vector_banks(k_out, 0)()
+                if k_out < SLOTS - 1:
                     turned_columns(k_out)
-                for a in range(SLOT_TILES):
-                    for first, width in ((0, BANK), (LAST_BANK, OUT - LAST_BANK)):
-                        finish = vector_bank(k_out, a, first, width)
-                        if plain or a == 0:
-                            finish()
-                            if k_out in EARLY:
-                                store(k_out, a, slice(first, first + width))
-                        else:
-                            waiting.append((finish, k_out, a, slice(first, first + width)))
+                else:
+                    straight_columns(k_out)
+                    store_turned(k_out)
+                waiting.append(vector_banks(k_out, 1))
             if k == 1:
                 for copy in bd_copies:
                     copy()
                 regroup_wd(nc.scalar.copy, BANK, BANK)
             if k == 2:
-                rotate_bias(1)
-                regroup_wd(nc.scalar.copy, 2 * BANK, BANK // 2)
-                regroup_wd(nc.vector.tensor_copy, 5 * BANK // 2, BANK // 2)
-            if k == 3:
-                quantise_wd(2)
+                regroup_wd(nc.scalar.copy, 2 * BANK, BANK)
+        for finish in waiting:
+            finish()

@@ -32,8 +32,10 @@ SLOTS = GROUPS * TILES // SLOT_TILES
 POSITIONS = GROUPS_PER_SEQUENCE * TILES
 BANK = 512
 OUT_BANKS = OUT // BANK
-VECTOR_COLS = 2 * BANK
-TURNED_BLOCKS = (OUT - VECTOR_COLS) // P
+VECTOR_COLS = 896
+SHARED = 256
+TURNED_BLOCKS = 3
+TURNED = VECTOR_COLS + SHARED
 RESULT_BUFS = 6
 VECTOR_BANKS = 4
 ROT_U = DR // 2
@@ -142,7 +144,7 @@ def tile_deepseekmla_pa_t_kernel(tc, x, W_c, b_c, W_d, b_d, out):
         def spread_bd_cols():
             acc = scalar_psum.tile([P, TURNED_BLOCKS, 32], F32, tag="bank")
             for block in range(TURNED_BLOCKS):
-                first = VECTOR_COLS + block * P
+                first = TURNED + block * P
                 nc.tensor.matmul(
                     acc[:, block, :], lhsT=bd_rows[:, first : first + P], rhs=ones[:, 0:32], start=True, stop=True
                 )
@@ -307,24 +309,49 @@ def tile_deepseekmla_pa_t_kernel(tc, x, W_c, b_c, W_d, b_d, out):
         def vector_banks(k, a):
             accs = []
             for first in range(0, VECTOR_COLS, BANK):
+                width = min(BANK, VECTOR_COLS - first)
                 acc = vector_psum.tile([P, BANK], F32, tag="bank")
-                token_product(acc[:], k, a, slice(first, first + BANK))
-                accs.append(acc)
+                done = 0
+                for part in (BANK, BANK // 2, P):
+                    if done + part <= width:
+                        token_product(acc[:, done : done + part], k, a, slice(first + done, first + done + part))
+                        done += part
+                accs.append((first, width, acc))
 
             def finish():
-                for i in range(len(accs)):
-                    cols = slice(i * BANK, (i + 1) * BANK)
-                    nc.vector.tensor_tensor(out=result[k][:, a, cols], in0=accs[i][:], in1=bd_all[:, cols], op=ADD)
+                for first, width, acc in accs:
+                    cols = slice(first, first + width)
+                    nc.vector.tensor_tensor(out=result[k][:, a, cols], in0=acc[:, 0:width], in1=bd_all[:, cols], op=ADD)
                 nc.sync.dma_start(out=out_rows(k)[:, a, 0:VECTOR_COLS], in_=result[k][:, a, 0:VECTOR_COLS])
 
             return finish
+
+        def both_tiles(psum, k, first, width):
+            acc = psum.tile([P, SLOT_TILES, 2 * P], F32, tag="bank")
+            for a in range(SLOT_TILES):
+                token_product(acc[:, a, 0:width], k, a, slice(first, first + width))
+            return acc[:, :, 0:width]
+
+        def add_bd(engine, k, first, width, in0):
+            cols = slice(first, first + width)
+            bias = bd_all[:, cols].unsqueeze(1).to_broadcast([P, SLOT_TILES, width])
+            engine.tensor_tensor(out=result[k][:, :, cols], in0=in0, in1=bias, op=ADD)
+
+        def shared_columns(k):
+            acc = both_tiles(scalar_psum, k, VECTOR_COLS, SHARED)
+            nc.scalar.copy(out=result[k][:, :, VECTOR_COLS:TURNED], in_=acc)
+
+        def finish_shared(k):
+            for first in range(VECTOR_COLS, TURNED, 256):
+                width = min(256, TURNED - first)
+                add_bd(nc.gpsimd, k, first, width, result[k][:, :, first : first + width])
 
         def turned_columns(k):
             sums[k] = work.tile([P, TURNED_BLOCKS, SPAN], F32, name="sums")
             for pair in range(0, TURNED_BLOCKS, 2):
                 acc = scalar_psum.tile([P, 2, SPAN], F32, tag="bank")
-                for i in range(2):
-                    first = VECTOR_COLS + (pair + i) * P
+                for i in range(min(2, TURNED_BLOCKS - pair)):
+                    first = TURNED + (pair + i) * P
                     channels = slice(first, first + P)
                     nc.tensor.matmul_mx(
                         out=acc[:, i],
@@ -335,7 +362,7 @@ def tile_deepseekmla_pa_t_kernel(tc, x, W_c, b_c, W_d, b_d, out):
                         start=True,
                         stop=True,
                     )
-                for i in range(2):
+                for i in range(min(2, TURNED_BLOCKS - pair)):
                     block = pair + i
                     nc.scalar.activation(
                         out=sums[k][:, block], in_=acc[:, i], func=IDENTITY, bias=bd_cols[:, block : block + 1]
@@ -345,21 +372,19 @@ def tile_deepseekmla_pa_t_kernel(tc, x, W_c, b_c, W_d, b_d, out):
             for pair in range(0, TURNED_BLOCKS, 2):
                 acc = scalar_psum.tile([P, SLOT_TILES, 2, P], F32, tag="bank")
                 for a in range(SLOT_TILES):
-                    for i in range(2):
+                    for i in range(min(2, TURNED_BLOCKS - pair)):
                         nc.tensor.transpose(acc[:, a, i, :], sums[k][:, pair + i, a * P : (a + 1) * P], ident[:])
-                first = VECTOR_COLS + pair * P
+                first = TURNED + pair * P
+                width = min(2, TURNED_BLOCKS - pair) * P
                 nc.scalar.copy(
-                    out=result[k][:, :, first : first + 2 * P], in_=acc[:].rearrange("p a i c -> p a (i c)")
+                    out=result[k][:, :, first : first + width], in_=acc[:].rearrange("p a i c -> p a (i c)")[:, :, 0:width]
                 )
 
         def straight_columns(k):
             for first in range(VECTOR_COLS, OUT, 2 * P):
-                cols = slice(first, first + 2 * P)
-                acc = vector_psum.tile([P, SLOT_TILES, 2 * P], F32, tag="bank")
-                for a in range(SLOT_TILES):
-                    token_product(acc[:, a], k, a, cols)
-                bias = bd_all[:, cols].unsqueeze(1).to_broadcast([P, SLOT_TILES, 2 * P])
-                nc.vector.tensor_tensor(out=result[k][:, :, cols], in0=acc[:], in1=bias, op=ADD)
+                width = min(2 * P, OUT - first)
+                acc = both_tiles(vector_psum, k, first, width)
+                add_bd(nc.vector, k, first, width, acc)
 
         def out_rows(k):
             first = k % 2 * SLOT_TILES
@@ -395,6 +420,9 @@ def tile_deepseekmla_pa_t_kernel(tc, x, W_c, b_c, W_d, b_d, out):
                 transpose_r(k_r)
             if 0 <= k_back < SLOTS - 1:
                 turn_back(k_back)
+            if 0 <= k_back < SLOTS - 1:
+                finish_shared(k_back)
+            if 0 <= k_back < SLOTS - 1:
                 store_turned(k_back)
             if k == R_LAG:
                 quantise_wd(0)
@@ -412,6 +440,7 @@ def tile_deepseekmla_pa_t_kernel(tc, x, W_c, b_c, W_d, b_d, out):
                 vector_banks(k_out, 0)()
                 if k_out < SLOTS - 1:
                     turned_columns(k_out)
+                    shared_columns(k_out)
                 else:
                     straight_columns(k_out)
                     store_turned(k_out)

@@ -33,15 +33,16 @@ POSITIONS = GROUPS_PER_SEQUENCE * TILES
 BANK = 512
 OUT_BANKS = OUT // BANK
 VECTOR_COLS = 896
-SHARED = 256
-TURNED_BLOCKS = 3
-TURNED = VECTOR_COLS + SHARED
+SHARED_COLS = 384
+TURNED_FIRST = VECTOR_COLS + SHARED_COLS
+TURNED_BLOCKS = (OUT - TURNED_FIRST) // P
+PAIR_COLS = 2 * P
 RESULT_BUFS = 6
 VECTOR_BANKS = 4
 ROT_U = DR // 2
 ROUND_MAGIC = 1.5 * 2.0**23
 C_LAG, R_LAG, OUT_LAG, BACK_LAG = 1, 3, 4, 5
-ORDERED = 6
+ORDERED = 5
 
 FLOPS = 2 * B * S * D * DC + 2 * B * S * DC * OUT
 
@@ -144,7 +145,7 @@ def tile_deepseekmla_pa_t_kernel(tc, x, W_c, b_c, W_d, b_d, out):
         def spread_bd_cols():
             acc = scalar_psum.tile([P, TURNED_BLOCKS, 32], F32, tag="bank")
             for block in range(TURNED_BLOCKS):
-                first = TURNED + block * P
+                first = TURNED_FIRST + block * P
                 nc.tensor.matmul(
                     acc[:, block, :], lhsT=bd_rows[:, first : first + P], rhs=ones[:, 0:32], start=True, stop=True
                 )
@@ -179,8 +180,8 @@ def tile_deepseekmla_pa_t_kernel(tc, x, W_c, b_c, W_d, b_d, out):
             )
 
         wc_grouped = consts.tile([P, DC, PACK], BF16, align_bytes=64)
-        wc_codes = consts.tile([P, DC], U32, align_bytes=64)
-        wc_scales = consts.tile([P, DC], U8, align_bytes=64)
+        wc_codes = consts.tile([P, DC], U32, align_bytes=256)
+        wc_scales = consts.tile([P, DC], U8, align_bytes=256)
 
         def prepare_wc():
             for u in range(2):
@@ -193,8 +194,8 @@ def tile_deepseekmla_pa_t_kernel(tc, x, W_c, b_c, W_d, b_d, out):
             )
 
         wd_grouped = consts.tile([P, OUT, PACK], BF16, align_bytes=64)
-        wd_codes = consts.tile([P, OUT], U32, align_bytes=64)
-        wd_scales = consts.tile([P, OUT], U8, align_bytes=64)
+        wd_codes = consts.tile([P, OUT], U32, align_bytes=256)
+        wd_scales = consts.tile([P, OUT], U8, align_bytes=256)
 
         def regroup_wd(copy, first, width):
             cols = slice(first, first + width)
@@ -246,8 +247,8 @@ def tile_deepseekmla_pa_t_kernel(tc, x, W_c, b_c, W_d, b_d, out):
 
         def quantise(k):
             parts = slice(0 if k < SLOTS else 1, 2 if k >= R_LAG else 1)
-            codes[k] = work.tile([P, 2, SPAN], U32, align_bytes=64, name="codes")
-            scales[k] = work.tile([P, 2, SPAN], U8, align_bytes=64, name="scales")
+            codes[k] = work.tile([P, 2, SPAN], U32, align_bytes=256, name="codes")
+            scales[k] = work.tile([P, 2, SPAN], U8, align_bytes=256, name="scales")
             nc.vector.quantize_mx(
                 out=codes[k][:, parts].rearrange("p s n -> p (s n)").bitcast(FP8X4),
                 scales=scales[k][:, parts].rearrange("p s n -> p (s n)"),
@@ -306,91 +307,84 @@ def tile_deepseekmla_pa_t_kernel(tc, x, W_c, b_c, W_d, b_d, out):
                 stop=True,
             )
 
+        def product_bank(k, a, first):
+            width = min(BANK, VECTOR_COLS - first)
+            acc = vector_psum.tile([P, BANK], F32, tag="bank")
+            done = 0
+            for part in (BANK, BANK // 2, BANK // 4):
+                if done + part <= width:
+                    token_product(acc[:, done : done + part], k, a, slice(first + done, first + done + part))
+                    done += part
+            return acc[:, 0:width], slice(first, first + width)
+
         def vector_banks(k, a):
-            accs = []
-            for first in range(0, VECTOR_COLS, BANK):
-                width = min(BANK, VECTOR_COLS - first)
-                acc = vector_psum.tile([P, BANK], F32, tag="bank")
-                done = 0
-                for part in (BANK, BANK // 2, P):
-                    if done + part <= width:
-                        token_product(acc[:, done : done + part], k, a, slice(first + done, first + done + part))
-                        done += part
-                accs.append((first, width, acc))
+            banks = [product_bank(k, a, first) for first in range(0, VECTOR_COLS, BANK)]
 
             def finish():
-                for first, width, acc in accs:
-                    cols = slice(first, first + width)
-                    nc.vector.tensor_tensor(out=result[k][:, a, cols], in0=acc[:, 0:width], in1=bd_all[:, cols], op=ADD)
-                nc.sync.dma_start(out=out_rows(k)[:, a, 0:VECTOR_COLS], in_=result[k][:, a, 0:VECTOR_COLS])
+                for acc, cols in banks:
+                    nc.vector.tensor_tensor(out=result[k][:, a, cols], in0=acc, in1=bd_all[:, cols], op=ADD)
+                cols = slice(0, VECTOR_COLS)
+                nc.sync.dma_start(out=out_rows(k)[:, a, cols], in_=result[k][:, a, cols])
 
             return finish
 
-        def both_tiles(psum, k, first, width):
-            acc = psum.tile([P, SLOT_TILES, 2 * P], F32, tag="bank")
+        def both_tiles(psum, k, cols):
+            acc = psum.tile([P, SLOT_TILES, PAIR_COLS], F32, tag="bank")
+            acc = acc[:, :, 0 : cols.stop - cols.start]
             for a in range(SLOT_TILES):
-                token_product(acc[:, a, 0:width], k, a, slice(first, first + width))
-            return acc[:, :, 0:width]
+                token_product(acc[:, a], k, a, cols)
+            return acc
 
-        def add_bd(engine, k, first, width, in0):
-            cols = slice(first, first + width)
-            bias = bd_all[:, cols].unsqueeze(1).to_broadcast([P, SLOT_TILES, width])
+        def add_bd(engine, k, cols, in0):
+            bias = bd_all[:, cols].unsqueeze(1).to_broadcast([P, SLOT_TILES, cols.stop - cols.start])
             engine.tensor_tensor(out=result[k][:, :, cols], in0=in0, in1=bias, op=ADD)
 
+        def pairs_of_columns(first, last):
+            return [slice(start, min(start + PAIR_COLS, last)) for start in range(first, last, PAIR_COLS)]
+
         def shared_columns(k):
-            acc = both_tiles(scalar_psum, k, VECTOR_COLS, SHARED)
-            nc.scalar.copy(out=result[k][:, :, VECTOR_COLS:TURNED], in_=acc)
+            for cols in pairs_of_columns(VECTOR_COLS, TURNED_FIRST):
+                nc.scalar.copy(out=result[k][:, :, cols], in_=both_tiles(scalar_psum, k, cols))
 
         def finish_shared(k):
-            for first in range(VECTOR_COLS, TURNED, 256):
-                width = min(256, TURNED - first)
-                add_bd(nc.gpsimd, k, first, width, result[k][:, :, first : first + width])
+            cols = slice(VECTOR_COLS, TURNED_FIRST)
+            add_bd(nc.gpsimd, k, cols, result[k][:, :, cols])
 
         def turned_columns(k):
             sums[k] = work.tile([P, TURNED_BLOCKS, SPAN], F32, name="sums")
-            for pair in range(0, TURNED_BLOCKS, 2):
-                acc = scalar_psum.tile([P, 2, SPAN], F32, tag="bank")
-                for i in range(min(2, TURNED_BLOCKS - pair)):
-                    first = TURNED + (pair + i) * P
-                    channels = slice(first, first + P)
-                    nc.tensor.matmul_mx(
-                        out=acc[:, i],
-                        lhsT=wd_codes[:, channels].bitcast(FP8X4),
-                        lhsT_scale=wd_scales[:, channels],
-                        rhs=codes[k + R_LAG][:, 1].bitcast(FP8X4),
-                        rhs_scale=scales[k + R_LAG][:, 1],
-                        start=True,
-                        stop=True,
-                    )
-                for i in range(min(2, TURNED_BLOCKS - pair)):
-                    block = pair + i
-                    nc.scalar.activation(
-                        out=sums[k][:, block], in_=acc[:, i], func=IDENTITY, bias=bd_cols[:, block : block + 1]
-                    )
-
-        def turn_back(k):
-            for pair in range(0, TURNED_BLOCKS, 2):
-                acc = scalar_psum.tile([P, SLOT_TILES, 2, P], F32, tag="bank")
-                for a in range(SLOT_TILES):
-                    for i in range(min(2, TURNED_BLOCKS - pair)):
-                        nc.tensor.transpose(acc[:, a, i, :], sums[k][:, pair + i, a * P : (a + 1) * P], ident[:])
-                first = TURNED + pair * P
-                width = min(2, TURNED_BLOCKS - pair) * P
-                nc.scalar.copy(
-                    out=result[k][:, :, first : first + width], in_=acc[:].rearrange("p a i c -> p a (i c)")[:, :, 0:width]
+            acc = scalar_psum.tile([P, TURNED_BLOCKS, SPAN], F32, tag="bank")
+            for block in range(TURNED_BLOCKS):
+                channels = slice(TURNED_FIRST + block * P, TURNED_FIRST + (block + 1) * P)
+                nc.tensor.matmul_mx(
+                    out=acc[:, block],
+                    lhsT=wd_codes[:, channels].bitcast(FP8X4),
+                    lhsT_scale=wd_scales[:, channels],
+                    rhs=codes[k + R_LAG][:, 1].bitcast(FP8X4),
+                    rhs_scale=scales[k + R_LAG][:, 1],
+                    start=True,
+                    stop=True,
+                )
+            for block in range(TURNED_BLOCKS):
+                nc.scalar.activation(
+                    out=sums[k][:, block], in_=acc[:, block], func=IDENTITY, bias=bd_cols[:, block : block + 1]
                 )
 
+        def turn_back(k):
+            acc = scalar_psum.tile([P, SLOT_TILES, TURNED_BLOCKS, P], F32, tag="bank")
+            for a in range(SLOT_TILES):
+                for block in range(TURNED_BLOCKS):
+                    nc.tensor.transpose(acc[:, a, block, :], sums[k][:, block, a * P : (a + 1) * P], ident[:])
+            nc.scalar.copy(out=result[k][:, :, TURNED_FIRST:OUT], in_=acc[:].rearrange("p a b c -> p a (b c)"))
+
         def straight_columns(k):
-            for first in range(VECTOR_COLS, OUT, 2 * P):
-                width = min(2 * P, OUT - first)
-                acc = both_tiles(vector_psum, k, first, width)
-                add_bd(nc.vector, k, first, width, acc)
+            for cols in pairs_of_columns(VECTOR_COLS, OUT):
+                add_bd(nc.vector, k, cols, both_tiles(vector_psum, k, cols))
 
         def out_rows(k):
             first = k % 2 * SLOT_TILES
             return out_groups[k // 2][:, first : first + SLOT_TILES, :]
 
-        def store_turned(k):
+        def store_rest(k):
             nc.sync.dma_start(out=out_rows(k)[:, :, VECTOR_COLS:OUT], in_=result[k][:, :, VECTOR_COLS:OUT])
 
         spread_bc()
@@ -420,10 +414,8 @@ def tile_deepseekmla_pa_t_kernel(tc, x, W_c, b_c, W_d, b_d, out):
                 transpose_r(k_r)
             if 0 <= k_back < SLOTS - 1:
                 turn_back(k_back)
-            if 0 <= k_back < SLOTS - 1:
                 finish_shared(k_back)
-            if 0 <= k_back < SLOTS - 1:
-                store_turned(k_back)
+                store_rest(k_back)
             if k == R_LAG:
                 quantise_wd(0)
                 quantise_wd(1)
@@ -443,7 +435,7 @@ def tile_deepseekmla_pa_t_kernel(tc, x, W_c, b_c, W_d, b_d, out):
                     shared_columns(k_out)
                 else:
                     straight_columns(k_out)
-                    store_turned(k_out)
+                    store_rest(k_out)
                 waiting.append(vector_banks(k_out, 1))
             if k == 1:
                 for copy in bd_copies:

import math
from contextlib import ExitStack

import concourse.mybir as mybir
from concourse.masks import make_identity

F32 = mybir.dt.float32
BF16 = mybir.dt.bfloat16
I32 = mybir.dt.int32
U32 = mybir.dt.uint32
U8 = mybir.dt.uint8
FP8X4 = mybir.dt.float8_e4m3fn_x4
ADD = mybir.AluOpType.add
SUBTRACT = mybir.AluOpType.subtract
MULT = mybir.AluOpType.mult
IDENTITY = mybir.ActivationFunctionType.Identity
SIN = mybir.ActivationFunctionType.Sin

B, S, D, DC, DR, OUT = 4, 1024, 512, 512, 64, 1536
HALF = DR // 2
ROPE_BASE = 10000.0

P = 128
PACK = 4
PAIR = 2
TILES = 4
GROUP = TILES * P
GROUPS = B * S // GROUP
GROUPS_PER_SEQUENCE = S // GROUP
SLOT_TILES = 2
SLOTS = GROUPS * TILES // SLOT_TILES
POSITIONS = GROUPS_PER_SEQUENCE * TILES
BANK = 512
OUT_BANKS = OUT // BANK
VECTOR_COLS = 896
SHARED_COLS = 384
TURNED_FIRST = VECTOR_COLS + SHARED_COLS
TURNED_BLOCKS = (OUT - TURNED_FIRST) // P
PAIR_COLS = 2 * P
RESULT_BUFS = 6
VECTOR_BANKS = 4
ROT_U = DR // 2
ROUND_MAGIC = 1.5 * 2.0**23
C_LAG, R_LAG, OUT_LAG, BACK_LAG = 1, 3, 4, 5
ORDERED = 5

FLOPS = 2 * B * S * D * DC + 2 * B * S * DC * OUT


def tile_deepseekmla_pa_t_kernel(tc, x, W_c, b_c, W_d, b_d, out):
    nc = tc.nc
    x_groups = x.flatten_outer_dims().rearrange("(g p a) d -> g p (a d)", p=P, a=TILES)
    out_groups = out.flatten_outer_dims().rearrange("(g p a) c -> g p a c", p=P, a=TILES)

    with ExitStack() as ctx:
        consts = ctx.enter_context(tc.tile_pool(name="consts", bufs=1))
        work = ctx.enter_context(tc.tile_pool(name="work", bufs=4))
        results = ctx.enter_context(tc.tile_pool(name="results", bufs=RESULT_BUFS))
        vector_psum = ctx.enter_context(tc.psum_pool(name="vector_psum", bufs=VECTOR_BANKS))
        scalar_psum = ctx.enter_context(tc.psum_pool(name="scalar_psum", bufs=8 - VECTOR_BANKS))
        ctx.enter_context(tc.manual_schedule())

        bc_rows = consts.tile([P, DC], BF16)
        nc.vector.memset(bc_rows[:].bitcast(I32), 0)
        nc.sync.dma_start(out=bc_rows[0:1, :], in_=b_c.unsqueeze(0))
        bd_rows = consts.tile([P, OUT], BF16)
        nc.vector.memset(bd_rows[:].bitcast(I32), 0)
        nc.sync.dma_start(out=bd_rows[0:1, :], in_=b_d.unsqueeze(0))
        wc_raw = consts.tile([P, PACK, DC], BF16)
        nc.sync.dma_start(out=wc_raw[:], in_=W_c.rearrange("(q k) c -> q k c", k=PACK))
        x_sb = []
        for g in range(GROUPS):
            x_sb.append(consts.tile([P, TILES * D], BF16, name="x_sb%d" % g))

        def load_x(g, first, tiles):
            cols = slice(first * D, (first + tiles) * D)
            nc.sync.dma_start(out=x_sb[g][:, cols], in_=x_groups[g][:, cols])

        for k in range(3):
            load_x(k // 2, k % 2 * SLOT_TILES, SLOT_TILES)
        wd_raw = consts.tile([P, PACK, OUT], BF16)
        wd_rows = W_d.rearrange("(p t) c -> p t c", t=PACK)
        for n in range(OUT_BANKS):
            cols = slice(n * BANK, (n + 1) * BANK)
            nc.sync.dma_start(out=wd_raw[:, :, cols], in_=wd_rows[:, :, cols])
        load_x(1, SLOT_TILES, SLOT_TILES)
        for g in range(2, GROUPS):
            load_x(g, 0, TILES)

        ones = consts.tile([P, P], BF16)
        nc.vector.memset(ones[:], 1.0)
        warm = consts.tile([P, 1], F32)
        nc.vector.memset(warm[:], 0.0)
        nc.scalar.activation(out=warm[:], in_=warm[:], func=SIN)
        position = consts.tile([P, POSITIONS, 1], I32)
        nc.gpsimd.iota(position[:], pattern=[[GROUP, GROUPS_PER_SEQUENCE], [1, TILES]], base=0, channel_multiplier=TILES)
        ident = consts.tile([P, P], F32)
        make_identity(nc, ident[:])
        turns = consts.tile([P, 2, POSITIONS, HALF], F32)
        for j in range(2 * PACK):
            column = 16 * (j // 2 % 2) + 2 * (j // 4) + j % 2
            nc.vector.tensor_scalar_mul(
                out=turns[:, 0, :, column : column + 1],
                in0=position[:],
                scalar1=1.0 / ROPE_BASE ** (2.0 * j / DR) / (2.0 * math.pi),
            )
        by_i = turns[:, 0].rearrange("p g (u c) -> p (g u) c", u=2)
        for i in (2, 4):
            nc.vector.tensor_scalar_mul(
                out=by_i[:, :, PAIR * i : 2 * PAIR * i],
                in0=by_i[:, :, 0 : PAIR * i],
                scalar1=1.0 / ROPE_BASE ** (2.0 * PACK * i / DR),
            )
        nc.vector.tensor_scalar_add(out=turns[:, 1], in0=turns[:, 0], scalar1=0.25)
        whole = consts.tile([P, 2, POSITIONS, HALF], F32)
        nc.vector.tensor_scalar(
            out=whole[:], in0=turns[:], scalar1=ROUND_MAGIC, scalar2=ROUND_MAGIC, op0=ADD, op1=SUBTRACT
        )
        nc.vector.tensor_tensor(out=turns[:], in0=turns[:], in1=whole[:], op=SUBTRACT)
        table = consts.tile([P, 2, POSITIONS, DR], F32)

        def fill_table():
            turn = 2.0 * math.pi
            for s, far, scale in ((0, 0, turn), (0, 1, turn), (1, 0, turn), (1, 1, -turn)):
                nc.scalar.activation(
                    out=table[:, s].rearrange("p g (u h i) -> p (g u) h i", u=2, h=2)[:, :, far, :],
                    in_=turns[:, 1 - s].rearrange("p g (u i) -> p (g u) i", u=2),
                    func=SIN,
                    scale=scale,
                )

        bc_cols = consts.tile([P, 2, 256], F32)
        bd_all = consts.tile([P, OUT], BF16)
        bd_cols = consts.tile([P, TURNED_BLOCKS], F32)

        def spread_bc():
            acc = scalar_psum.tile([P, BANK], F32, tag="bank")
            nc.tensor.matmul(acc[:], lhsT=ones[:], rhs=bc_rows[:], start=True, stop=True)
            for u in range(2):
                nc.scalar.copy(
                    out=bc_cols[:, u].rearrange("n (p e) -> n p e", e=PAIR),
                    in_=acc[:].rearrange("n (p u e) -> n u p e", u=2, e=PAIR)[:, u],
                )

        def spread_bd_cols():
            acc = scalar_psum.tile([P, TURNED_BLOCKS, 32], F32, tag="bank")
            for block in range(TURNED_BLOCKS):
                first = TURNED_FIRST + block * P
                nc.tensor.matmul(
                    acc[:, block, :], lhsT=bd_rows[:, first : first + P], rhs=ones[:, 0:32], start=True, stop=True
                )
            nc.scalar.copy(out=bd_cols[:], in_=acc[:, :, 0])

        def spread_bd(n):
            cols = slice(n * BANK, (n + 1) * BANK)
            acc = vector_psum.tile([P, BANK], F32, tag="bank")
            nc.tensor.matmul(acc[:], lhsT=ones[:], rhs=bd_rows[:, cols], start=True, stop=True)
            return lambda: nc.scalar.copy(out=bd_all[:, cols], in_=acc[:])

        rotated_bias = consts.tile([P, POSITIONS, DR], F32)
        bias_part = consts.tile([P, POSITIONS, DR], F32)

        def swapped(cols):
            return cols.rearrange("n t (h i) -> n t h i", h=2)[:, :, ::-1, :]

        def rotate_bias():
            for s, into in ((0, rotated_bias), (1, bias_part)):
                nc.vector.tensor_tensor(
                    out=into[:].rearrange("n a (u c) -> n a u c", u=2),
                    in0=table[:, s].rearrange("n a (u c) -> n a u c", u=2),
                    in1=bc_cols[:, :, 0:ROT_U].unsqueeze(1).to_broadcast([P, POSITIONS, 2, ROT_U]),
                    op=MULT,
                )
            total = rotated_bias[:].rearrange("n a (u c) -> n (a u) c", u=2)
            nc.vector.tensor_tensor(
                out=total.rearrange("n t (h i) -> n t h i", h=2),
                in0=total.rearrange("n t (h i) -> n t h i", h=2),
                in1=swapped(bias_part[:].rearrange("n a (u c) -> n (a u) c", u=2)),
                op=ADD,
            )

        wc_grouped = consts.tile([P, DC, PACK], BF16, align_bytes=64)
        wc_codes = consts.tile([P, DC], U32, align_bytes=256)
        wc_scales = consts.tile([P, DC], U8, align_bytes=256)

        def prepare_wc():
            for u in range(2):
                nc.vector.tensor_copy(
                    out=wc_grouped[:, u * 256 : (u + 1) * 256, :].rearrange("q (p e) k -> q p k e", e=PAIR),
                    in_=wc_raw[:].rearrange("q k (p u e) -> q u p k e", u=2, e=PAIR)[:, u],
                )
            nc.vector.quantize_mx(
                out=wc_codes[:].bitcast(FP8X4), scales=wc_scales[:], in_=wc_grouped[:].rearrange("q c k -> q (c k)")
            )

        wd_grouped = consts.tile([P, OUT, PACK], BF16, align_bytes=64)
        wd_codes = consts.tile([P, OUT], U32, align_bytes=256)
        wd_scales = consts.tile([P, OUT], U8, align_bytes=256)

        def regroup_wd(copy, first, width):
            cols = slice(first, first + width)
            copy(
                out=wd_grouped[:, cols, :].rearrange("p (c i) t -> p c t i", i=4),
                in_=wd_raw[:, :, cols].rearrange("p t (c i) -> p c t i", i=4),
            )

        def quantise_wd(n):
            cols = slice(n * BANK, (n + 1) * BANK)
            nc.vector.quantize_mx(
                out=wd_codes[:, cols].bitcast(FP8X4),
                scales=wd_scales[:, cols],
                in_=wd_grouped[:, cols, :].rearrange("p c t -> p (c t)"),
            )

        SPAN = SLOT_TILES * P
        x_words, grouped, codes, scales, products, r_rows, sums, result = {}, {}, {}, {}, {}, {}, {}, {}

        def turn_words(k, part, words):
            turned = scalar_psum.tile([P, SLOT_TILES, 2, P], F32, tag="bank")
            for a in range(SLOT_TILES):
                for u in range(2):
                    nc.tensor.transpose(turned[:, a, u, :], words[a][u], ident[:])
            nc.scalar.copy(
                out=grouped[k][:, part].bitcast(F32).rearrange("p (a n u) -> p a n u", a=SLOT_TILES, u=2),
                in_=turned[:].rearrange("p a u n -> p a n u"),
            )

        def words_of_x(k):
            first = k % 2 * SLOT_TILES * D
            return x_sb[k // 2][:, first : first + SLOT_TILES * D].bitcast(F32)

        def order_words(k):
            x_words[k] = work.tile([P, SLOT_TILES, 2, P], F32, name="x_words")
            nc.scalar.copy(out=x_words[k][:], in_=words_of_x(k).rearrange("n (a q u) -> n a u q", a=SLOT_TILES, u=2))

        def transpose_x(k):
            if k < ORDERED:
                words = words_of_x(k).rearrange("n (a q u) -> n a u q", a=SLOT_TILES, u=2)
            else:
                words = x_words[k]
            turn_words(k, 0, [[words[:, a, u, :] for u in range(2)] for a in range(SLOT_TILES)])

        def transpose_r(k):
            words = r_rows[k][:].rearrange("n a u c -> n (a u c)").bitcast(F32)
            words = words.rearrange("n (a u q) -> n a u q", a=SLOT_TILES, u=2)
            turn_words(k + R_LAG, 1, [[words[:, a, u, :] for u in range(2)] for a in range(SLOT_TILES)])

        def quantise(k):
            parts = slice(0 if k < SLOTS else 1, 2 if k >= R_LAG else 1)
            codes[k] = work.tile([P, 2, SPAN], U32, align_bytes=256, name="codes")
            scales[k] = work.tile([P, 2, SPAN], U8, align_bytes=256, name="scales")
            nc.vector.quantize_mx(
                out=codes[k][:, parts].rearrange("p s n -> p (s n)").bitcast(FP8X4),
                scales=scales[k][:, parts].rearrange("p s n -> p (s n)"),
                in_=grouped[k][:, parts].rearrange("p s n -> p (s n)"),
            )

        def first_product(k, a):
            at = (k * SLOT_TILES + a) % POSITIONS
            tokens = slice(a * P, (a + 1) * P)
            c_acc = vector_psum.tile([P, 2, 256], F32, tag="bank")
            nc.tensor.matmul_mx(
                out=c_acc[:].rearrange("n u c -> n (u c)"),
                lhsT=codes[k][:, 0, tokens].bitcast(FP8X4),
                lhsT_scale=scales[k][:, 0, tokens],
                rhs=wc_codes[:].bitcast(FP8X4),
                rhs_scale=wc_scales[:],
                start=True,
                stop=True,
            )
            nc.vector.tensor_tensor(
                out=products[k][:, :, a],
                in0=c_acc[:, :, 0:ROT_U].unsqueeze(1).to_broadcast([P, 2, 2, ROT_U]),
                in1=table[:, :, at, :].rearrange("n s (u c) -> n s u c", u=2),
                op=MULT,
            )
            nc.vector.tensor_tensor(
                out=r_rows[k][:, a, :, ROT_U:256], in0=c_acc[:, :, ROT_U:256], in1=bc_cols[:, :, ROT_U:256], op=ADD
            )

        def rotate(k):
            at = k * SLOT_TILES % POSITIONS
            own = products[k][:, 0].rearrange("n a u c -> n (a u) c")
            nc.gpsimd.tensor_tensor(
                out=own.rearrange("n t (h i) -> n t h i", h=2),
                in0=own.rearrange("n t (h i) -> n t h i", h=2),
                in1=swapped(products[k][:, 1].rearrange("n a u c -> n (a u) c")),
                op=ADD,
            )
            nc.gpsimd.tensor_tensor(
                out=r_rows[k][:, :, :, 0:ROT_U],
                in0=products[k][:, 0],
                in1=rotated_bias[:, at : at + SLOT_TILES, :].rearrange("n a (u c) -> n a u c", u=2),
                op=ADD,
            )


        def token_product(acc, k, a, cols):
            tokens = slice(a * P, (a + 1) * P)
            nc.tensor.matmul_mx(
                out=acc,
                lhsT=codes[k + R_LAG][:, 1, tokens].bitcast(FP8X4),
                lhsT_scale=scales[k + R_LAG][:, 1, tokens],
                rhs=wd_codes[:, cols].bitcast(FP8X4),
                rhs_scale=wd_scales[:, cols],
                start=True,
                stop=True,
            )

        def product_bank(k, a, first):
            width = min(BANK, VECTOR_COLS - first)
            acc = vector_psum.tile([P, BANK], F32, tag="bank")
            done = 0
            for part in (BANK, BANK // 2, BANK // 4):
                if done + part <= width:
                    token_product(acc[:, done : done + part], k, a, slice(first + done, first + done + part))
                    done += part
            return acc[:, 0:width], slice(first, first + width)

        def vector_banks(k, a):
            banks = [product_bank(k, a, first) for first in range(0, VECTOR_COLS, BANK)]

            def finish():
                for acc, cols in banks:
                    nc.vector.tensor_tensor(out=result[k][:, a, cols], in0=acc, in1=bd_all[:, cols], op=ADD)
                cols = slice(0, VECTOR_COLS)
                nc.sync.dma_start(out=out_rows(k)[:, a, cols], in_=result[k][:, a, cols])

            return finish

        def both_tiles(psum, k, cols):
            acc = psum.tile([P, SLOT_TILES, PAIR_COLS], F32, tag="bank")
            acc = acc[:, :, 0 : cols.stop - cols.start]
            for a in range(SLOT_TILES):
                token_product(acc[:, a], k, a, cols)
            return acc

        def add_bd(engine, k, cols, in0):
            bias = bd_all[:, cols].unsqueeze(1).to_broadcast([P, SLOT_TILES, cols.stop - cols.start])
            engine.tensor_tensor(out=result[k][:, :, cols], in0=in0, in1=bias, op=ADD)

        def pairs_of_columns(first, last):
            return [slice(start, min(start + PAIR_COLS, last)) for start in range(first, last, PAIR_COLS)]

        def shared_columns(k):
            for cols in pairs_of_columns(VECTOR_COLS, TURNED_FIRST):
                nc.scalar.copy(out=result[k][:, :, cols], in_=both_tiles(scalar_psum, k, cols))

        def finish_shared(k):
            cols = slice(VECTOR_COLS, TURNED_FIRST)
            add_bd(nc.gpsimd, k, cols, result[k][:, :, cols])

        def turned_columns(k):
            sums[k] = work.tile([P, TURNED_BLOCKS, SPAN], F32, name="sums")
            acc = scalar_psum.tile([P, TURNED_BLOCKS, SPAN], F32, tag="bank")
            for block in range(TURNED_BLOCKS):
                channels = slice(TURNED_FIRST + block * P, TURNED_FIRST + (block + 1) * P)
                nc.tensor.matmul_mx(
                    out=acc[:, block],
                    lhsT=wd_codes[:, channels].bitcast(FP8X4),
                    lhsT_scale=wd_scales[:, channels],
                    rhs=codes[k + R_LAG][:, 1].bitcast(FP8X4),
                    rhs_scale=scales[k + R_LAG][:, 1],
                    start=True,
                    stop=True,
                )
            for block in range(TURNED_BLOCKS):
                nc.scalar.activation(
                    out=sums[k][:, block], in_=acc[:, block], func=IDENTITY, bias=bd_cols[:, block : block + 1]
                )

        def turn_back(k):
            acc = scalar_psum.tile([P, SLOT_TILES, TURNED_BLOCKS, P], F32, tag="bank")
            for a in range(SLOT_TILES):
                for block in range(TURNED_BLOCKS):
                    nc.tensor.transpose(acc[:, a, block, :], sums[k][:, block, a * P : (a + 1) * P], ident[:])
            nc.scalar.copy(out=result[k][:, :, TURNED_FIRST:OUT], in_=acc[:].rearrange("p a b c -> p a (b c)"))

        def straight_columns(k):
            for cols in pairs_of_columns(VECTOR_COLS, OUT):
                add_bd(nc.vector, k, cols, both_tiles(vector_psum, k, cols))

        def out_rows(k):
            first = k % 2 * SLOT_TILES
            return out_groups[k // 2][:, first : first + SLOT_TILES, :]

        def store_rest(k):
            nc.sync.dma_start(out=out_rows(k)[:, :, VECTOR_COLS:OUT], in_=result[k][:, :, VECTOR_COLS:OUT])

        spread_bc()
        spread_bd_cols()
        bd_copies = [spread_bd(n) for n in range(OUT_BANKS)]
        fill_table()
        prepare_wc()
        waiting = []
        for k in range(SLOTS + BACK_LAG):
            k_c, k_r, k_out, k_back = k - C_LAG, k - R_LAG, k - OUT_LAG, k - BACK_LAG
            if 1 <= k <= SLOTS - 1 + OUT_LAG:
                quantise(k - 1)
            if k == OUT_LAG:
                quantise_wd(2)
            if k == C_LAG:
                rotate_bias()
            for finish in waiting:
                finish()
            waiting = []
            if k == 2:
                regroup_wd(nc.vector.tensor_copy, 0, BANK)
            if k < SLOTS + R_LAG:
                grouped[k] = work.tile([P, 2, SPAN * PACK], BF16, align_bytes=64, name="grouped")
            if k < SLOTS:
                transpose_x(k)
            if 0 <= k_r < SLOTS:
                transpose_r(k_r)
            if 0 <= k_back < SLOTS - 1:
                turn_back(k_back)
                finish_shared(k_back)
                store_rest(k_back)
            if k == R_LAG:
                quantise_wd(0)
                quantise_wd(1)
            if ORDERED <= k + 2 < SLOTS:
                order_words(k + 2)
            if 0 <= k_c < SLOTS:
                r_rows[k_c] = work.tile([P, SLOT_TILES, 2, 256], BF16, name="r_rows")
                products[k_c] = work.tile([P, 2, SLOT_TILES, 2, ROT_U], F32, name="products")
                for a in range(SLOT_TILES):
                    first_product(k_c, a)
                rotate(k_c)
            if 0 <= k_out < SLOTS:
                result[k_out] = results.tile([P, SLOT_TILES, OUT], F32, name="result")
                vector_banks(k_out, 0)()
                if k_out < SLOTS - 1:
                    turned_columns(k_out)
                    shared_columns(k_out)
                else:
                    straight_columns(k_out)
                    store_rest(k_out)
                waiting.append(vector_banks(k_out, 1))
            if k == 1:
                for copy in bd_copies:
                    copy()
                regroup_wd(nc.scalar.copy, BANK, BANK)
            if k == 2:
                regroup_wd(nc.scalar.copy, 2 * BANK, BANK)
        for finish in waiting:
            finish()
